import numpy as np
import ml_dtypes


def mxq(x, axis, fmt="e4m3"):
    dtype, down = {"e4m3": (ml_dtypes.float8_e4m3fn, 7), "e5m2": (ml_dtypes.float8_e5m2, 14)}[fmt]
    v = np.moveaxis(np.asarray(x, np.float32).astype(ml_dtypes.bfloat16).astype(np.float64), axis, -1)
    blocks = v.reshape(v.shape[:-1] + (-1, 32))
    amax = np.abs(blocks).max(-1, keepdims=True)
    byte = np.maximum(np.where(amax > 0, np.frexp(amax)[1] - 1 + 127, 0) - down, 1)
    scale = np.exp2(byte - 127.0)
    codes = (blocks / scale).astype(np.float32).astype(dtype).astype(np.float64)
    return np.moveaxis((codes * scale).reshape(v.shape), -1, axis)


WIDE = False


def mx_kscale(k):
    if not WIDE:
        return np.ones(k)
    levels = np.array([10, -10, 5, -5, 0])
    a = np.random.permutation(np.resize(levels, k // 512 * 4)).reshape(k // 512, 4)
    idx = np.arange(k)
    return np.exp2(a[idx // 512, idx % 128 // 32])


BF16 = ml_dtypes.bfloat16


def bf(x):
    return np.asarray(x, np.float32).astype(BF16)


def f64(x):
    return np.asarray(x).astype(np.float64)


E2M1 = np.array([0.0, 0.5, 1.0, 1.5, 2.0, 3.0, 4.0, 6.0, -0.0, -0.5, -1.0, -1.5, -2.0, -3.0, -4.0, -6.0])


def pack_weight(w, fmt):
    k, n = w.shape
    w = f64(bf(w)).reshape(k // 32, 32, n)
    amax = np.abs(w).max(1)
    if fmt == "e4m3":
        byte = np.frexp(amax)[1] - 1 + 127 - 7
    else:
        mant, ex = np.frexp(amax / 6.0)
        byte = np.where(mant > 0.5, ex, ex - 1) + 127
    byte = np.clip(np.where(amax > 0, byte, 1), 1, 254)
    scaled = (w * np.exp2(127.0 - byte)[:, None, :]).reshape(k, n).astype(np.float32)
    by_word = np.ascontiguousarray(scaled.reshape(k // 512, 128, 4, n).transpose(0, 1, 3, 2))
    if fmt == "e4m3":
        words = by_word.astype(ml_dtypes.float8_e4m3fn).view(np.uint8)
    else:
        c = by_word.astype(ml_dtypes.float4_e2m1fn).view(np.uint8) & 0xF
        words = c[..., 0::2] | (c[..., 1::2] << 4)
    return np.ascontiguousarray(words), np.ascontiguousarray(byte.astype(np.uint8).reshape(k // 512, 16, n))


def unpack_weight(words, scales, fmt):
    g, p, n, _ = words.shape
    if fmt == "e4m3":
        vals = np.ascontiguousarray(words).view(ml_dtypes.float8_e4m3fn).astype(np.float64)
    else:
        nib = np.empty((g, p, n, 4), np.uint8)
        nib[..., 0::2] = words & 0xF
        nib[..., 1::2] = words >> 4
        vals = E2M1[nib]
    vals = vals * np.repeat(np.exp2(scales.astype(np.float64) - 127.0), 8, axis=1)[..., None]
    return vals.transpose(0, 1, 3, 2).reshape(g * 512, n)

def pack4(w):
    words, scales = pack_weight(w, "e2m1")
    return words.reshape(words.shape[0], 128, -1), scales


def unpack4(words, scales):
    return unpack_weight(words.reshape(words.shape[0], 128, -1, 2), scales, "e2m1")


B, CL, CH, CK, CV, CO, H, W = 2, 1024, 2048, 256, 512, 1024, 48, 72
N = H * W
PSP = (1, 3, 6, 8)
EPS = 1e-5


def psp(x):
    b, c, h, w = x.shape
    return np.concatenate(
        [x.reshape(b, c, s, h // s, s, w // s).mean(axis=(3, 5)).reshape(b, c, s * s) for s in PSP], axis=2)


def setup_inputs():
    s = mx_kscale(CL)
    low_feats = bf(np.random.standard_normal((B, CL, H, W)) * s[None, :, None, None])
    wk = np.random.standard_normal((CK, CL)) * 2.5 / np.sqrt(CL) / s[None, :]
    wk_words, wk_scales = pack4(np.ascontiguousarray(wk.T))
    bk = bf(np.random.standard_normal(CK) * 0.3)
    gk = bf(np.random.uniform(0.5, 1.5, CK))
    bek = bf(np.random.standard_normal(CK) * 0.3)
    mk = bf(np.random.standard_normal(CK) * 0.3)
    vk = bf(np.random.uniform(0.5, 1.5, CK))
    wv = np.random.standard_normal((CV, CL)) * 3.0 / np.sqrt(CL) / s[None, :]
    wv_words, wv_scales = pack4(np.ascontiguousarray(wv.T))
    bv = bf(np.random.standard_normal(CV) * 0.3)
    return {"low_feats": low_feats,
            "wk_words": wk_words,
            "wk_scales": wk_scales,
            "bk": bk,
            "gk": gk,
            "bek": bek,
            "mk": mk,
            "vk": vk,
            "wv_words": wv_words,
            "wv_scales": wv_scales,
            "bv": bv}


def reference(low_feats, wk_words, wk_scales, bk, gk, bek, mk, vk, wv_words, wv_scales, bv):
    xq = mxq(f64(low_feats).reshape(B, CL, N), 1, "e4m3")
    v = (unpack4(wv_words, wv_scales).T @ xq) + f64(bv)[None, :, None]
    value = psp(v.reshape(B, CV, H, W)).transpose(0, 2, 1)
    u = (unpack4(wk_words, wk_scales).T @ xq) + f64(bk)[None, :, None]
    sc = f64(gk) / np.sqrt(f64(vk) + EPS)
    r = np.maximum((u - f64(mk)[None, :, None]) * sc[None, :, None] + f64(bek)[None, :, None], 0.0)
    key = psp(r.reshape(B, CK, H, W))
    return value, key

@@ -1,0 +1,380 @@
+from contextlib import ExitStack
+
+import concourse.mybir as mybir
+from concourse.masks import make_identity
+
+F32 = mybir.dt.float32
+BF16 = mybir.dt.bfloat16
+I32 = mybir.dt.int32
+U32 = mybir.dt.uint32
+U8 = mybir.dt.uint8
+FP8X4 = mybir.dt.float8_e4m3fn_x4
+FP4X4 = mybir.dt.float4_e2m1fn_x4
+ALU = mybir.AluOpType
+ACT = mybir.ActivationFunctionType
+AXIS = mybir.AxisListType
+
+B, CL, CK, CV, H, W = 2, 1024, 256, 512, 48, 72
+GRIDS = (1, 3, 6, 8)
+LOCATIONS = 1 + 9 + 36 + 64
+EPS = 1e-5
+
+P = 128
+PACK = 4
+GROUPS = CL // (P * PACK)
+
+CELL_H, CELL_W = 2, 3
+PLANES = CELL_H * CELL_W
+SIDE = H // CELL_H
+PAIR_PX = CELL_H * W
+PAIRS = B * SIDE
+
+UNIT = P
+N_UNITS = PAIRS * SIDE // UNIT
+CHUNK_PAIRS = 16
+CHUNK_CELLS = CHUNK_PAIRS * SIDE
+CHUNK_UNITS = CHUNK_CELLS // UNIT
+N_CHUNKS = PAIRS // CHUNK_PAIRS
+UNITS_OF_BATCH = 5
+MAX_PAIRS = 6
+
+K_TILES = CK // P
+LOOKAHEAD = 2
+
+FLOPS = 2 * (CK + CV) * CL * B * H * W
+
+
+def first_pair(j):
+    rows = -(-UNIT * j // SIDE)
+    return min(rows + rows % 2, CHUNK_PAIRS)
+
+
+def load_weight(nc, words, scales, words_sb, scales_sb):
+    nc.sync.dma_start(out=words_sb[:].bitcast(I32), in_=words.rearrange("g p n -> p g n").bitcast(I32))
+    for quad in range(4):
+        nc.sync.dma_start(
+            out=scales_sb[32 * quad : 32 * quad + 4].bitcast(I32),
+            in_=scales[:, 4 * quad : 4 * quad + 4, :].rearrange("g r n -> r g n").bitcast(I32),
+        )
+
+
+def build_pool_weights(nc, pool, pool_w):
+    edges_r, edges_c = PAIRS + 1, SIDE + 1
+    index_i = pool.tile([P, N_UNITS + edges_r + edges_c], I32)
+    nc.gpsimd.iota(index_i[:, 0:N_UNITS], pattern=[[UNIT, N_UNITS]], base=0, channel_multiplier=1)
+    nc.gpsimd.iota(
+        index_i[:, N_UNITS : N_UNITS + edges_r], pattern=[[SIDE, edges_r]], base=0, channel_multiplier=0
+    )
+    nc.gpsimd.iota(index_i[:, N_UNITS + edges_r :], pattern=[[1, edges_c]], base=0, channel_multiplier=0)
+    index = pool.tile([P, N_UNITS + edges_r + edges_c], F32)
+    nc.vector.tensor_copy(out=index[:], in_=index_i[:])
+    cell = index[:, 0:N_UNITS]
+    row_start = index[:, N_UNITS : N_UNITS + edges_r]
+    col_edge = index[:, N_UNITS + edges_r :]
+
+    reached_r = pool.tile([P, N_UNITS, edges_r], F32)
+    nc.vector.tensor_tensor(
+        out=reached_r[:],
+        in0=cell.unsqueeze(2).to_broadcast([P, N_UNITS, edges_r]),
+        in1=row_start.unsqueeze(1).to_broadcast([P, N_UNITS, edges_r]),
+        op=ALU.is_ge,
+    )
+    row = pool.tile([P, N_UNITS], F32)
+    nc.vector.tensor_reduce(out=row[:], in_=reached_r[:, :, 1:edges_r], axis=AXIS.X, op=ALU.add)
+    col = pool.tile([P, N_UNITS], F32)
+    nc.vector.scalar_tensor_tensor(
+        out=col[:], in0=row[:], scalar=-float(SIDE), in1=cell, op0=ALU.mult, op1=ALU.add
+    )
+    reached_c = pool.tile([P, N_UNITS, edges_c], F32)
+    nc.vector.tensor_tensor(
+        out=reached_c[:],
+        in0=col[:].unsqueeze(2).to_broadcast([P, N_UNITS, edges_c]),
+        in1=col_edge.unsqueeze(1).to_broadcast([P, N_UNITS, edges_c]),
+        op=ALU.is_ge,
+    )
+
+    nc.vector.memset(pool_w[:], 0.0)
+    offset = 0
+    for s in GRIDS:
+        step = SIDE // s
+        row_hot = pool.tile([P, N_UNITS, B * s], F32, name="row_hot%d" % s)
+        nc.vector.tensor_sub(
+            out=row_hot[:], in0=reached_r[:, :, 0:PAIRS:step], in1=reached_r[:, :, step : PAIRS + 1 : step]
+        )
+        col_hot = pool.tile([P, N_UNITS, s], F32, name="col_hot%d" % s)
+        nc.vector.tensor_sub(
+            out=col_hot[:], in0=reached_c[:, :, 0:SIDE:step], in1=reached_c[:, :, step : SIDE + 1 : step]
+        )
+        col_share = pool.tile([P, N_UNITS, s], F32, name="col_share%d" % s)
+        nc.vector.tensor_scalar_mul(out=col_share[:], in0=col_hot[:], scalar1=1.0 / ((H // s) * (W // s)))
+        for b in range(B):
+            units = slice((UNITS_OF_BATCH - 1) * b, (UNITS_OF_BATCH - 1) * b + UNITS_OF_BATCH)
+            shape = [P, UNITS_OF_BATCH, s, s]
+            nc.vector.tensor_tensor(
+                out=pool_w[:, UNITS_OF_BATCH * b : UNITS_OF_BATCH * (b + 1), offset : offset + s * s].rearrange(
+                    "p u (i j) -> p u i j", j=s
+                ),
+                in0=row_hot[:, units, s * b : s * (b + 1)].unsqueeze(3).to_broadcast(shape),
+                in1=col_share[:, units, :].unsqueeze(2).to_broadcast(shape),
+                op=ALU.mult,
+            )
+        offset += s * s
+
+
+def tile_afnb_pa_t_kernel(
+    tc, low_feats, wk_words, wk_scales, bk, gk, bek, mk, vk, wv_words, wv_scales, bv, out_0, out_1
+):
+    nc = tc.nc
+    with ExitStack() as ctx:
+        consts = ctx.enter_context(tc.tile_pool(name="consts", bufs=1))
+        raw_pool = ctx.enter_context(tc.tile_pool(name="raw", bufs=LOOKAHEAD + 1))
+        work = ctx.enter_context(tc.tile_pool(name="work", bufs=2))
+        k_psum = ctx.enter_context(tc.psum_pool(name="k_psum", bufs=4))
+        v_psum = ctx.enter_context(tc.psum_pool(name="v_psum", bufs=2))
+        value_psum = ctx.enter_context(tc.psum_pool(name="value_psum", bufs=B))
+
+        x_rows = low_feats.rearrange(
+            "b (g p t) (r i) w -> b g p t r (i w)", g=GROUPS, p=P, t=PACK, i=CELL_H
+        )
+
+        def load(u):
+            q, j = divmod(u, CHUNK_UNITS)
+            first = CHUNK_PAIRS * q + first_pair(j)
+            last = CHUNK_PAIRS * q + first_pair(j + 1)
+            tiles = []
+            for g in range(GROUPS):
+                raw = raw_pool.tile([P, PACK, MAX_PAIRS, PAIR_PX], BF16, name="raw%d" % g)
+                for b in range(B):
+                    lo, hi = max(first, SIDE * b), min(last, SIDE * (b + 1))
+                    if lo < hi:
+                        nc.sync.dma_start(
+                            out=raw[:, :, lo - first : hi - first, :],
+                            in_=x_rows[b, g, :, :, lo - SIDE * b : hi - SIDE * b, :],
+                        )
+                tiles.append(raw)
+            return tiles
+
+        raws = {}
+        raws[0] = load(0)
+
+        wk_w = consts.tile([P, GROUPS, 2 * CK], U8, align_bytes=64)
+        wv_w = consts.tile([P, GROUPS, 2 * CV], U8, align_bytes=64)
+        wk_s = consts.tile([P, GROUPS, CK], U8, align_bytes=64)
+        wv_s = consts.tile([P, GROUPS, CV], U8, align_bytes=64)
+        nc.vector.memset(wk_s[:].bitcast(I32), 0)
+        nc.vector.memset(wv_s[:].bitcast(I32), 0)
+        load_weight(nc, wk_words, wk_scales, wk_w, wk_s)
+        load_weight(nc, wv_words, wv_scales, wv_w, wv_s)
+
+        vectors = (bk, gk, bek, mk, vk)
+        rows_sb = consts.tile([P, P], BF16)
+        nc.vector.memset(rows_sb[:], 0.0)
+        for n, vector in enumerate(vectors):
+            nc.scalar.dma_start(
+                out=rows_sb[K_TILES * n : K_TILES * (n + 1), :], in_=vector.rearrange("(m c) -> m c", m=K_TILES)
+            )
+        identity = consts.tile([P, P], BF16)
+        make_identity(nc, identity[:])
+        cols_ps = k_psum.tile([P, P], BF16, name="cols_ps", tag="k_acc")
+        nc.tensor.transpose(out=cols_ps[:], in_=rows_sb[:], identity=identity[:])
+        cols = consts.tile([P, len(vectors), K_TILES], F32)
+        nc.vector.tensor_copy(
+            out=cols[:].rearrange("p n m -> p (n m)"), in_=cols_ps[:, 0 : len(vectors) * K_TILES]
+        )
+        bk_c, gk_c, bek_c, mk_c, vk_c = (cols[:, n, :] for n in range(len(vectors)))
+        var_eps = consts.tile([P, K_TILES], F32)
+        nc.vector.tensor_scalar_add(out=var_eps[:], in0=vk_c, scalar1=EPS)
+        std = consts.tile([P, K_TILES], F32)
+        nc.scalar.sqrt(out=std[:], in_=var_eps[:])
+        inv_std = consts.tile([P, K_TILES], F32)
+        nc.vector.reciprocal(out=inv_std[:], in_=std[:])
+        gain = consts.tile([P, K_TILES], F32)
+        nc.vector.tensor_mul(out=gain[:], in0=gk_c, in1=inv_std[:])
+        centred = consts.tile([P, K_TILES], F32)
+        nc.vector.tensor_sub(out=centred[:], in0=bk_c, in1=mk_c)
+        scaled = consts.tile([P, K_TILES], F32)
+        nc.vector.tensor_mul(out=scaled[:], in0=centred[:], in1=gain[:])
+        shift = consts.tile([P, K_TILES], F32)
+        nc.vector.tensor_add(out=shift[:], in0=scaled[:], in1=bek_c)
+
+        bv_row = consts.tile([P, CV], BF16)
+        nc.vector.memset(bv_row[:], 0.0)
+        nc.scalar.dma_start(out=bv_row[0:1, :], in_=bv.rearrange("(o c) -> o c", o=1))
+        ones = consts.tile([P, P], BF16)
+        nc.vector.memset(ones[:], 1.0)
+        bv_ps = k_psum.tile([P, CV], F32, name="bv_ps", tag="k_acc")
+        nc.tensor.matmul(out=bv_ps[:], lhsT=ones[:], rhs=bv_row[:], start=True, stop=True)
+        bv_all = consts.tile([P, CV], F32)
+        nc.vector.tensor_copy(out=bv_all[:], in_=bv_ps[:])
+
+        for u in range(1, LOOKAHEAD):
+            raws[u] = load(u)
+
+        grouped = [
+            consts.tile([P, PLANES, CHUNK_CELLS, PACK], BF16, name="grouped%d" % g, align_bytes=64)
+            for g in range(GROUPS)
+        ]
+        codes = consts.tile([P, GROUPS, N_CHUNKS, PLANES, CHUNK_CELLS], U32, align_bytes=64)
+        x_scales = consts.tile([P, GROUPS, N_CHUNKS, PLANES, CHUNK_CELLS], U8, align_bytes=64)
+        pool_w = consts.tile([P, B * UNITS_OF_BATCH, P], F32)
+        k_cells = consts.tile([P, K_TILES, PAIRS * SIDE], F32)
+        k_strips = {s: consts.tile([P, PAIRS, K_TILES, s], F32, name="k_strips%d" % s) for s in (8, 6)}
+        value_acc = {}
+
+        def regroup_and_quantise(u):
+            q, j = divmod(u, CHUNK_UNITS)
+            lo, hi = first_pair(j), first_pair(j + 1)
+            cells = slice(SIDE * lo, SIDE * hi)
+            for g in range(GROUPS):
+                raw = raws[u][g]
+                nc.vector.tensor_copy(
+                    out=grouped[g][:, 0:CELL_W, cells, :].rearrange("p k (r c) t -> p r c t k", c=SIDE),
+                    in_=raw[:, :, 0 : hi - lo, 0:W].rearrange("p t r (c k) -> p r c t k", k=CELL_W),
+                )
+                for k in range(CELL_W):
+                    nc.scalar.copy(
+                        out=grouped[g][:, CELL_W + k, cells, :].rearrange("p (r c) t -> p r c t", c=SIDE),
+                        in_=raw[:, :, 0 : hi - lo, W + k : PAIR_PX : CELL_W].rearrange("p t r c -> p r c t"),
+                    )
+            unit = slice(UNIT * j, UNIT * (j + 1))
+            for g in range(GROUPS):
+                for i in range(PLANES):
+                    nc.vector.quantize_mx(
+                        out=codes[:, g, q, i, unit].bitcast(FP8X4),
+                        scales=x_scales[:, g, q, i, unit],
+                        in_=grouped[g][:, i, unit, :].rearrange("p c t -> p (c t)"),
+                    )
+
+        def key_unit(u):
+            q, j = divmod(u, CHUNK_UNITS)
+            unit = slice(UNIT * j, UNIT * (j + 1))
+            r = work.tile([P, K_TILES, PLANES, UNIT], F32, name="r")
+            for m in range(K_TILES):
+                for i_r in range(CELL_H):
+                    k_acc = k_psum.tile([P, CELL_W, UNIT], F32, name="k_acc")
+                    for i_c in range(CELL_W):
+                        i = CELL_W * i_r + i_c
+                        for g in range(GROUPS):
+                            nc.tensor.matmul_mx(
+                                out=k_acc[:, i_c, :],
+                                lhsT=wk_w[:, g, 2 * P * m : 2 * P * (m + 1)].bitcast(FP4X4),
+                                lhsT_scale=wk_s[:, g, P * m : P * (m + 1)],
+                                rhs=codes[:, g, q, i, unit].bitcast(FP8X4),
+                                rhs_scale=x_scales[:, g, q, i, unit],
+                                start=(g == 0),
+                                stop=(g == GROUPS - 1),
+                            )
+                    nc.scalar.activation(
+                        out=r[:, m, CELL_W * i_r : CELL_W * (i_r + 1), :],
+                        in_=k_acc[:],
+                        func=ACT.Relu,
+                        bias=shift[:, m : m + 1],
+                        scale=gain[:, m : m + 1],
+                    )
+            both_rows = work.tile([P, K_TILES, CELL_W, UNIT], F32, name="both_rows")
+            nc.vector.tensor_add(out=both_rows[:], in0=r[:, :, 0:CELL_W, :], in1=r[:, :, CELL_W:PLANES, :])
+            two_cols = work.tile([P, K_TILES, UNIT], F32, name="two_cols")
+            nc.vector.tensor_add(out=two_cols[:], in0=both_rows[:, :, 0, :], in1=both_rows[:, :, 1, :])
+            nc.vector.tensor_add(
+                out=k_cells[:, :, UNIT * u : UNIT * (u + 1)], in0=two_cols[:], in1=both_rows[:, :, 2, :]
+            )
+
+        def value_unit(u):
+            q, j = divmod(u, CHUNK_UNITS)
+            unit = slice(UNIT * j, UNIT * (j + 1))
+            v_acc = v_psum.tile([P, CV], F32, name="v_acc")
+            for i in range(PLANES):
+                for g in range(GROUPS):
+                    nc.tensor.matmul_mx(
+                        out=v_acc[:],
+                        lhsT=codes[:, g, q, i, unit].bitcast(FP8X4),
+                        lhsT_scale=x_scales[:, g, q, i, unit],
+                        rhs=wv_w[:, g, :].bitcast(FP4X4),
+                        rhs_scale=wv_s[:, g, :],
+                        start=(i == 0 and g == 0),
+                        stop=(i == PLANES - 1 and g == GROUPS - 1),
+                    )
+            v_cells = work.tile([P, CV], F32, name="v_cells")
+            nc.scalar.copy(out=v_cells[:], in_=v_acc[:])
+            for b in range(B):
+                n = u - (UNITS_OF_BATCH - 1) * b
+                if 0 <= n < UNITS_OF_BATCH:
+                    if n == 0:
+                        value_acc[b] = value_psum.tile([P, CV], F32, name="value_acc")
+                    nc.tensor.matmul(
+                        out=value_acc[b][:],
+                        lhsT=pool_w[:, UNITS_OF_BATCH * b + n, :],
+                        rhs=v_cells[:],
+                        start=(n == 0),
+                        stop=(n == UNITS_OF_BATCH - 1),
+                    )
+
+        def key_strips(q):
+            for s, strips in k_strips.items():
+                nc.vector.tensor_reduce(
+                    out=strips[:, CHUNK_PAIRS * q : CHUNK_PAIRS * (q + 1), :, :].rearrange("p r m j -> p m r j"),
+                    in_=k_cells[:, :, CHUNK_CELLS * q : CHUNK_CELLS * (q + 1)].rearrange(
+                        "p m (r j k) -> p m r j k", j=s, k=SIDE // s
+                    ),
+                    axis=AXIS.X,
+                    op=ALU.add,
+                )
+
+        def finish_batch(b):
+            value_sb = work.tile([P, CV], F32, name="value_sb")
+            nc.vector.tensor_add(out=value_sb[:], in0=value_acc[b][:], in1=bv_all[:])
+            nc.sync.dma_start(out=out_0[b], in_=value_sb[0:LOCATIONS, :])
+
+            sums = {s: work.tile([P, s, K_TILES, s], F32, name="sums%d" % s) for s in GRIDS}
+            for s, strips in k_strips.items():
+                nc.vector.tensor_reduce(
+                    out=sums[s][:].rearrange("p i m j -> p i (m j)"),
+                    in_=strips[:, SIDE * b : SIDE * (b + 1), :, :].rearrange(
+                        "p (i k) m j -> p i (m j) k", k=SIDE // s
+                    ),
+                    axis=AXIS.X,
+                    op=ALU.add,
+                )
+            halves = work.tile([P, 6, K_TILES, 3], F32, name="halves")
+            nc.vector.tensor_reduce(
+                out=halves[:], in_=sums[6][:].rearrange("p i m (j k) -> p i m j k", k=2), axis=AXIS.X, op=ALU.add
+            )
+            nc.vector.tensor_reduce(
+                out=sums[3][:].rearrange("p i m j -> p i (m j)"),
+                in_=halves[:].rearrange("p (i k) m j -> p i (m j) k", k=2),
+                axis=AXIS.X,
+                op=ALU.add,
+            )
+            nc.vector.tensor_reduce(
+                out=sums[1][:].rearrange("p i m j -> p (i m j)"),
+                in_=sums[3][:].rearrange("p i m j -> p m i j"),
+                axis=AXIS.XY,
+                op=ALU.add,
+            )
+            key_sb = work.tile([P, K_TILES, LOCATIONS], F32, name="key_sb")
+            offset = 0
+            for s in GRIDS:
+                nc.vector.tensor_scalar_mul(
+                    out=key_sb[:, :, offset : offset + s * s].rearrange("p m (i j) -> p m i j", j=s),
+                    in0=sums[s][:].rearrange("p i m j -> p m i j"),
+                    scalar1=1.0 / ((H // s) * (W // s)),
+                )
+                offset += s * s
+            nc.sync.dma_start(out=out_1[b].rearrange("(m c) l -> c m l", m=K_TILES), in_=key_sb[:])
+
+        for u in range(N_UNITS + 1):
+            if u + LOOKAHEAD < N_UNITS:
+                raws[u + LOOKAHEAD] = load(u + LOOKAHEAD)
+            if u < N_UNITS:
+                regroup_and_quantise(u)
+            if u == 0:
+                build_pool_weights(nc, consts, pool_w)
+            else:
+                done = u - 1
+                key_unit(done)
+                value_unit(done)
+                q, j = divmod(done, CHUNK_UNITS)
+                if j == CHUNK_UNITS - 1:
+                    key_strips(q)
+                    if q >= 1:
+                        finish_batch(q - 1)

@@ -227,14 +227,14 @@ def tile_afnb_pa_t_kernel(
             cells = slice(SIDE * lo, SIDE * hi)
             for g in range(GROUPS):
                 raw = raws[u][g]
-                nc.vector.tensor_copy(
-                    out=grouped[g][:, 0:CELL_W, cells, :].rearrange("p k (r c) t -> p r c t k", c=SIDE),
-                    in_=raw[:, :, 0 : hi - lo, 0:W].rearrange("p t r (c k) -> p r c t k", k=CELL_W),
-                )
-                for k in range(CELL_W):
-                    nc.scalar.copy(
-                        out=grouped[g][:, CELL_W + k, cells, :].rearrange("p (r c) t -> p r c t", c=SIDE),
-                        in_=raw[:, :, 0 : hi - lo, W + k : PAIR_PX : CELL_W].rearrange("p t r c -> p r c t"),
+                for i_r, copy in enumerate((nc.vector.tensor_copy, nc.scalar.copy)):
+                    copy(
+                        out=grouped[g][:, CELL_W * i_r : CELL_W * (i_r + 1), cells, :].rearrange(
+                            "p k (r c) t -> p r c t k", c=SIDE
+                        ),
+                        in_=raw[:, :, 0 : hi - lo, W * i_r : W * (i_r + 1)].rearrange(
+                            "p t r (c k) -> p r c t k", k=CELL_W
+                        ),
                     )
             unit = slice(UNIT * j, UNIT * (j + 1))
             for g in range(GROUPS):

@@ -40,6 +40,7 @@ MAX_PAIRS = 6
 
 K_TILES = CK // P
 LOOKAHEAD = 2
+UPPER, LOWER = 0, 1
 
 FLOPS = 2 * (CK + CV) * CL * B * H * W
 
@@ -93,7 +94,7 @@ def build_pool_weights(nc, pool, pool_w):
         op=ALU.is_ge,
     )
 
-    nc.vector.memset(pool_w[:], 0.0)
+    nc.vector.memset(pool_w[:, :, LOCATIONS:P], 0.0)
     offset = 0
     for s in GRIDS:
         step = SIDE // s
@@ -129,9 +130,11 @@ def tile_afnb_pa_t_kernel(
         consts = ctx.enter_context(tc.tile_pool(name="consts", bufs=1))
         raw_pool = ctx.enter_context(tc.tile_pool(name="raw", bufs=LOOKAHEAD + 1))
         work = ctx.enter_context(tc.tile_pool(name="work", bufs=2))
+        relu_pool = ctx.enter_context(tc.tile_pool(name="relu", bufs=3))
         k_psum = ctx.enter_context(tc.psum_pool(name="k_psum", bufs=4))
         v_psum = ctx.enter_context(tc.psum_pool(name="v_psum", bufs=2))
         value_psum = ctx.enter_context(tc.psum_pool(name="value_psum", bufs=B))
+        ctx.enter_context(tc.manual_schedule())
 
         x_rows = low_feats.rearrange(
             "b (g p t) (r i) w -> b g p t r (i w)", g=GROUPS, p=P, t=PACK, i=CELL_H
@@ -154,8 +157,7 @@ def tile_afnb_pa_t_kernel(
                 tiles.append(raw)
             return tiles
 
-        raws = {}
-        raws[0] = load(0)
+        raws = {0: load(0)}
 
         wk_w = consts.tile([P, GROUPS, 2 * CK], U8, align_bytes=64)
         wv_w = consts.tile([P, GROUPS, 2 * CV], U8, align_bytes=64)
@@ -165,50 +167,58 @@ def tile_afnb_pa_t_kernel(
         nc.vector.memset(wv_s[:].bitcast(I32), 0)
         load_weight(nc, wk_words, wk_scales, wk_w, wk_s)
         load_weight(nc, wv_words, wv_scales, wv_w, wv_s)
+        for u in range(1, LOOKAHEAD):
+            raws[u] = load(u)
 
         vectors = (bk, gk, bek, mk, vk)
         rows_sb = consts.tile([P, P], BF16)
         nc.vector.memset(rows_sb[:], 0.0)
+        bv_row = consts.tile([P, CV], BF16)
+        nc.vector.memset(bv_row[:], 0.0)
+        ones = consts.tile([P, P], BF16)
+        nc.vector.memset(ones[:], 1.0)
         for n, vector in enumerate(vectors):
             nc.scalar.dma_start(
                 out=rows_sb[K_TILES * n : K_TILES * (n + 1), :], in_=vector.rearrange("(m c) -> m c", m=K_TILES)
             )
+        nc.scalar.dma_start(out=bv_row[0:1, :], in_=bv.rearrange("(o c) -> o c", o=1))
+        warm = consts.tile([P, 1], F32)
+        nc.scalar.sqrt(out=warm[:], in_=ones[:, 0:1])
+
+        pool_w = consts.tile([P, B * UNITS_OF_BATCH, P], F32)
+        build_pool_weights(nc, consts, pool_w)
         identity = consts.tile([P, P], BF16)
         make_identity(nc, identity[:])
+
         cols_ps = k_psum.tile([P, P], BF16, name="cols_ps", tag="k_acc")
         nc.tensor.transpose(out=cols_ps[:], in_=rows_sb[:], identity=identity[:])
-        cols = consts.tile([P, len(vectors), K_TILES], F32)
-        nc.vector.tensor_copy(
-            out=cols[:].rearrange("p n m -> p (n m)"), in_=cols_ps[:, 0 : len(vectors) * K_TILES]
-        )
-        bk_c, gk_c, bek_c, mk_c, vk_c = (cols[:, n, :] for n in range(len(vectors)))
-        var_eps = consts.tile([P, K_TILES], F32)
-        nc.vector.tensor_scalar_add(out=var_eps[:], in0=vk_c, scalar1=EPS)
-        std = consts.tile([P, K_TILES], F32)
-        nc.scalar.sqrt(out=std[:], in_=var_eps[:])
-        inv_std = consts.tile([P, K_TILES], F32)
-        nc.vector.reciprocal(out=inv_std[:], in_=std[:])
-        gain = consts.tile([P, K_TILES], F32)
-        nc.vector.tensor_mul(out=gain[:], in0=gk_c, in1=inv_std[:])
-        centred = consts.tile([P, K_TILES], F32)
-        nc.vector.tensor_sub(out=centred[:], in0=bk_c, in1=mk_c)
-        scaled = consts.tile([P, K_TILES], F32)
-        nc.vector.tensor_mul(out=scaled[:], in0=centred[:], in1=gain[:])
-        shift = consts.tile([P, K_TILES], F32)
-        nc.vector.tensor_add(out=shift[:], in0=scaled[:], in1=bek_c)
-
-        bv_row = consts.tile([P, CV], BF16)
-        nc.vector.memset(bv_row[:], 0.0)
-        nc.scalar.dma_start(out=bv_row[0:1, :], in_=bv.rearrange("(o c) -> o c", o=1))
-        ones = consts.tile([P, P], BF16)
-        nc.vector.memset(ones[:], 1.0)
         bv_ps = k_psum.tile([P, CV], F32, name="bv_ps", tag="k_acc")
         nc.tensor.matmul(out=bv_ps[:], lhsT=ones[:], rhs=bv_row[:], start=True, stop=True)
-        bv_all = consts.tile([P, CV], F32)
-        nc.vector.tensor_copy(out=bv_all[:], in_=bv_ps[:])
 
-        for u in range(1, LOOKAHEAD):
-            raws[u] = load(u)
+        std = consts.tile([P, K_TILES], F32)
+        gain = consts.tile([P, K_TILES], F32)
+        shift = consts.tile([P, K_TILES], F32)
+        bv_all = consts.tile([P, CV], F32)
+
+        def standard_deviation():
+            vk_at = K_TILES * (len(vectors) - 1)
+            nc.scalar.activation(out=std[:], in_=cols_ps[:, vk_at : vk_at + K_TILES], func=ACT.Sqrt, bias=EPS)
+
+        def finish_small_vectors():
+            cols = consts.tile([P, len(vectors), K_TILES], F32)
+            nc.vector.tensor_copy(
+                out=cols[:].rearrange("p n m -> p (n m)"), in_=cols_ps[:, 0 : len(vectors) * K_TILES]
+            )
+            bk_c, gk_c, bek_c, mk_c = (cols[:, n, :] for n in range(4))
+            inv_std = consts.tile([P, K_TILES], F32)
+            nc.vector.reciprocal(out=inv_std[:], in_=std[:])
+            centred = consts.tile([P, K_TILES], F32)
+            nc.vector.tensor_sub(out=centred[:], in0=bk_c, in1=mk_c)
+            nc.vector.tensor_mul(out=gain[:], in0=gk_c, in1=inv_std[:])
+            scaled = consts.tile([P, K_TILES], F32)
+            nc.vector.tensor_mul(out=scaled[:], in0=centred[:], in1=gain[:])
+            nc.vector.tensor_add(out=shift[:], in0=scaled[:], in1=bek_c)
+            nc.scalar.copy(out=bv_all[:], in_=bv_ps[:])
 
         grouped = [
             consts.tile([P, PLANES, CHUNK_CELLS, PACK], BF16, name="grouped%d" % g, align_bytes=64)
@@ -216,77 +226,74 @@ def tile_afnb_pa_t_kernel(
         ]
         codes = consts.tile([P, GROUPS, N_CHUNKS, PLANES, CHUNK_CELLS], U32, align_bytes=64)
         x_scales = consts.tile([P, GROUPS, N_CHUNKS, PLANES, CHUNK_CELLS], U8, align_bytes=64)
-        pool_w = consts.tile([P, B * UNITS_OF_BATCH, P], F32)
         k_cells = consts.tile([P, K_TILES, PAIRS * SIDE], F32)
         k_strips = {s: consts.tile([P, PAIRS, K_TILES, s], F32, name="k_strips%d" % s) for s in (8, 6)}
-        value_acc = {}
+        k_accs, relus, v_accs, v_cells, value_acc = {}, {}, {}, {}, {}
 
-        def regroup_and_quantise(u):
+        def where(u):
             q, j = divmod(u, CHUNK_UNITS)
+            return q, slice(UNIT * j, UNIT * (j + 1))
+
+        def regroup(u, g):
+            j = u % CHUNK_UNITS
             lo, hi = first_pair(j), first_pair(j + 1)
-            cells = slice(SIDE * lo, SIDE * hi)
-            for g in range(GROUPS):
-                raw = raws[u][g]
-                for i_r, copy in enumerate((nc.vector.tensor_copy, nc.scalar.copy)):
-                    copy(
-                        out=grouped[g][:, CELL_W * i_r : CELL_W * (i_r + 1), cells, :].rearrange(
-                            "p k (r c) t -> p r c t k", c=SIDE
-                        ),
-                        in_=raw[:, :, 0 : hi - lo, W * i_r : W * (i_r + 1)].rearrange(
-                            "p t r (c k) -> p r c t k", k=CELL_W
-                        ),
-                    )
-            unit = slice(UNIT * j, UNIT * (j + 1))
-            for g in range(GROUPS):
-                for i in range(PLANES):
-                    nc.vector.quantize_mx(
-                        out=codes[:, g, q, i, unit].bitcast(FP8X4),
-                        scales=x_scales[:, g, q, i, unit],
-                        in_=grouped[g][:, i, unit, :].rearrange("p c t -> p (c t)"),
-                    )
+            for i_r, copy in enumerate((nc.vector.tensor_copy, nc.scalar.copy)):
+                copy(
+                    out=grouped[g][:, CELL_W * i_r : CELL_W * (i_r + 1), SIDE * lo : SIDE * hi, :].rearrange(
+                        "p k (r c) t -> p r c t k", c=SIDE
+                    ),
+                    in_=raws[u][g][:, :, 0 : hi - lo, W * i_r : W * (i_r + 1)].rearrange(
+                        "p t r (c k) -> p r c t k", k=CELL_W
+                    ),
+                )
 
-        def key_unit(u):
-            q, j = divmod(u, CHUNK_UNITS)
-            unit = slice(UNIT * j, UNIT * (j + 1))
-            r = work.tile([P, K_TILES, PLANES, UNIT], F32, name="r")
+        def quantise(u, i_r, g):
+            q, unit = where(u)
+            for i in range(CELL_W * i_r, CELL_W * (i_r + 1)):
+                nc.vector.quantize_mx(
+                    out=codes[:, g, q, i, unit].bitcast(FP8X4),
+                    scales=x_scales[:, g, q, i, unit],
+                    in_=grouped[g][:, i, unit, :].rearrange("p c t -> p (c t)"),
+                )
+
+        def key_matmuls(u, i_r):
+            q, unit = where(u)
             for m in range(K_TILES):
-                for i_r in range(CELL_H):
-                    k_acc = k_psum.tile([P, CELL_W, UNIT], F32, name="k_acc")
-                    for i_c in range(CELL_W):
-                        i = CELL_W * i_r + i_c
-                        for g in range(GROUPS):
-                            nc.tensor.matmul_mx(
-                                out=k_acc[:, i_c, :],
-                                lhsT=wk_w[:, g, 2 * P * m : 2 * P * (m + 1)].bitcast(FP4X4),
-                                lhsT_scale=wk_s[:, g, P * m : P * (m + 1)],
-                                rhs=codes[:, g, q, i, unit].bitcast(FP8X4),
-                                rhs_scale=x_scales[:, g, q, i, unit],
-                                start=(g == 0),
-                                stop=(g == GROUPS - 1),
-                            )
-                    nc.scalar.activation(
-                        out=r[:, m, CELL_W * i_r : CELL_W * (i_r + 1), :],
-                        in_=k_acc[:],
-                        func=ACT.Relu,
-                        bias=shift[:, m : m + 1],
-                        scale=gain[:, m : m + 1],
-                    )
-            both_rows = work.tile([P, K_TILES, CELL_W, UNIT], F32, name="both_rows")
-            nc.vector.tensor_add(out=both_rows[:], in0=r[:, :, 0:CELL_W, :], in1=r[:, :, CELL_W:PLANES, :])
-            two_cols = work.tile([P, K_TILES, UNIT], F32, name="two_cols")
-            nc.vector.tensor_add(out=two_cols[:], in0=both_rows[:, :, 0, :], in1=both_rows[:, :, 1, :])
-            nc.vector.tensor_add(
-                out=k_cells[:, :, UNIT * u : UNIT * (u + 1)], in0=two_cols[:], in1=both_rows[:, :, 2, :]
-            )
+                k_acc = k_psum.tile([P, CELL_W, UNIT], F32, name="k_acc")
+                for i_c in range(CELL_W):
+                    i = CELL_W * i_r + i_c
+                    for g in range(GROUPS):
+                        nc.tensor.matmul_mx(
+                            out=k_acc[:, i_c, :],
+                            lhsT=wk_w[:, g, 2 * P * m : 2 * P * (m + 1)].bitcast(FP4X4),
+                            lhsT_scale=wk_s[:, g, P * m : P * (m + 1)],
+                            rhs=codes[:, g, q, i, unit].bitcast(FP8X4),
+                            rhs_scale=x_scales[:, g, q, i, unit],
+                            start=(g == 0),
+                            stop=(g == GROUPS - 1),
+                        )
+                k_accs[u, i_r, m] = k_acc
 
-        def value_unit(u):
-            q, j = divmod(u, CHUNK_UNITS)
-            unit = slice(UNIT * j, UNIT * (j + 1))
-            v_acc = v_psum.tile([P, CV], F32, name="v_acc")
-            for i in range(PLANES):
+        def key_relu(u, i_r):
+            if i_r == 0:
+                relus[u] = relu_pool.tile([P, K_TILES, PLANES, UNIT], F32, name="relu")
+            for m in range(K_TILES):
+                nc.scalar.activation(
+                    out=relus[u][:, m, CELL_W * i_r : CELL_W * (i_r + 1), :],
+                    in_=k_accs[u, i_r, m][:],
+                    func=ACT.Relu,
+                    bias=shift[:, m : m + 1],
+                    scale=gain[:, m : m + 1],
+                )
+
+        def value_matmuls(u, i_r):
+            q, unit = where(u)
+            if i_r == 0:
+                v_accs[u] = v_psum.tile([P, CV], F32, name="v_acc")
+            for i in range(CELL_W * i_r, CELL_W * (i_r + 1)):
                 for g in range(GROUPS):
                     nc.tensor.matmul_mx(
-                        out=v_acc[:],
+                        out=v_accs[u][:],
                         lhsT=codes[:, g, q, i, unit].bitcast(FP8X4),
                         lhsT_scale=x_scales[:, g, q, i, unit],
                         rhs=wv_w[:, g, :].bitcast(FP4X4),
@@ -294,8 +301,12 @@ def tile_afnb_pa_t_kernel(
                         start=(i == 0 and g == 0),
                         stop=(i == PLANES - 1 and g == GROUPS - 1),
                     )
-            v_cells = work.tile([P, CV], F32, name="v_cells")
-            nc.scalar.copy(out=v_cells[:], in_=v_acc[:])
+
+        def value_copy(u):
+            v_cells[u] = work.tile([P, CV], F32, name="v_cells")
+            nc.scalar.copy(out=v_cells[u][:], in_=v_accs[u][:])
+
+        def value_pool(u):
             for b in range(B):
                 n = u - (UNITS_OF_BATCH - 1) * b
                 if 0 <= n < UNITS_OF_BATCH:
@@ -304,27 +315,29 @@ def tile_afnb_pa_t_kernel(
                     nc.tensor.matmul(
                         out=value_acc[b][:],
                         lhsT=pool_w[:, UNITS_OF_BATCH * b + n, :],
-                        rhs=v_cells[:],
+                        rhs=v_cells[u][:],
                         start=(n == 0),
                         stop=(n == UNITS_OF_BATCH - 1),
                     )
 
-        def key_strips(q):
+        def key_strips(u):
+            first, last = UNIT * u // SIDE, UNIT * (u + 1) // SIDE
             for s, strips in k_strips.items():
                 nc.vector.tensor_reduce(
-                    out=strips[:, CHUNK_PAIRS * q : CHUNK_PAIRS * (q + 1), :, :].rearrange("p r m j -> p m r j"),
-                    in_=k_cells[:, :, CHUNK_CELLS * q : CHUNK_CELLS * (q + 1)].rearrange(
+                    out=strips[:, first:last, :, :].rearrange("p r m j -> p m r j"),
+                    in_=k_cells[:, :, SIDE * first : SIDE * last].rearrange(
                         "p m (r j k) -> p m r j k", j=s, k=SIDE // s
                     ),
                     axis=AXIS.X,
                     op=ALU.add,
                 )
 
-        def finish_batch(b):
+        def finish_value(b):
             value_sb = work.tile([P, CV], F32, name="value_sb")
             nc.vector.tensor_add(out=value_sb[:], in0=value_acc[b][:], in1=bv_all[:])
             nc.sync.dma_start(out=out_0[b], in_=value_sb[0:LOCATIONS, :])
 
+        def finish_key(b):
             sums = {s: work.tile([P, s, K_TILES, s], F32, name="sums%d" % s) for s in GRIDS}
             for s, strips in k_strips.items():
                 nc.vector.tensor_reduce(
@@ -362,19 +375,50 @@ def tile_afnb_pa_t_kernel(
                 offset += s * s
             nc.sync.dma_start(out=out_1[b].rearrange("(m c) l -> c m l", m=K_TILES), in_=key_sb[:])
 
-        for u in range(N_UNITS + 1):
-            if u + LOOKAHEAD < N_UNITS:
-                raws[u + LOOKAHEAD] = load(u + LOOKAHEAD)
-            if u < N_UNITS:
-                regroup_and_quantise(u)
-            if u == 0:
-                build_pool_weights(nc, consts, pool_w)
-            else:
-                done = u - 1
-                key_unit(done)
-                value_unit(done)
-                q, j = divmod(done, CHUNK_UNITS)
-                if j == CHUNK_UNITS - 1:
-                    key_strips(q)
-                    if q >= 1:
-                        finish_batch(q - 1)
+        for n in range(N_UNITS + 2):
+            new, last, before_last = n < N_UNITS, 1 <= n <= N_UNITS, n >= 2
+            if n + LOOKAHEAD < N_UNITS:
+                raws[n + LOOKAHEAD] = load(n + LOOKAHEAD)
+            if new:
+                regroup(n, 0)
+            if n == 0:
+                standard_deviation()
+            if new:
+                regroup(n, 1)
+            if n == 0:
+                finish_small_vectors()
+            if last:
+                key_relu(n - 1, LOWER)
+                value_copy(n - 1)
+            if new:
+                quantise(n, UPPER, 0)
+                quantise(n, UPPER, 1)
+                key_matmuls(n, UPPER)
+                key_relu(n, UPPER)
+                value_matmuls(n, UPPER)
+            if last:
+                value_pool(n - 1)
+            if before_last:
+                relu = relus[n - 2]
+                both_rows = work.tile([P, K_TILES, CELL_W, UNIT], F32, name="both_rows")
+                nc.vector.tensor_add(
+                    out=both_rows[:], in0=relu[:, :, 0:CELL_W, :], in1=relu[:, :, CELL_W:PLANES, :]
+                )
+            if new:
+                quantise(n, LOWER, 0)
+            if before_last:
+                two_cols = work.tile([P, K_TILES, UNIT], F32, name="two_cols")
+                nc.vector.tensor_add(out=two_cols[:], in0=both_rows[:, :, 0, :], in1=both_rows[:, :, 1, :])
+            if new:
+                quantise(n, LOWER, 1)
+                key_matmuls(n, LOWER)
+                value_matmuls(n, LOWER)
+            if before_last:
+                nc.vector.tensor_add(
+                    out=k_cells[:, :, UNIT * (n - 2) : UNIT * (n - 1)], in0=two_cols[:], in1=both_rows[:, :, 2, :]
+                )
+                key_strips(n - 2)
+                q, j = divmod(n - 2, CHUNK_UNITS)
+                if j == CHUNK_UNITS - 1 and q >= 1:
+                    finish_value(q - 1)
+                    finish_key(q - 1)

@@ -192,13 +192,10 @@ def tile_afnb_pa_t_kernel(
 
         cols_ps = k_psum.tile([P, P], BF16, name="cols_ps", tag="k_acc")
         nc.tensor.transpose(out=cols_ps[:], in_=rows_sb[:], identity=identity[:])
-        bv_ps = k_psum.tile([P, CV], F32, name="bv_ps", tag="k_acc")
-        nc.tensor.matmul(out=bv_ps[:], lhsT=ones[:], rhs=bv_row[:], start=True, stop=True)
 
         std = consts.tile([P, K_TILES], F32)
         gain = consts.tile([P, K_TILES], F32)
         shift = consts.tile([P, K_TILES], F32)
-        bv_all = consts.tile([P, CV], F32)
 
         def standard_deviation():
             vk_at = K_TILES * (len(vectors) - 1)
@@ -218,7 +215,6 @@ def tile_afnb_pa_t_kernel(
             scaled = consts.tile([P, K_TILES], F32)
             nc.vector.tensor_mul(out=scaled[:], in0=centred[:], in1=gain[:])
             nc.vector.tensor_add(out=shift[:], in0=scaled[:], in1=bek_c)
-            nc.scalar.copy(out=bv_all[:], in_=bv_ps[:])
 
         grouped = [
             consts.tile([P, PLANES, CHUNK_CELLS, PACK], BF16, name="grouped%d" % g, align_bytes=64)
@@ -228,7 +224,7 @@ def tile_afnb_pa_t_kernel(
         x_scales = consts.tile([P, GROUPS, N_CHUNKS, PLANES, CHUNK_CELLS], U8, align_bytes=64)
         k_cells = consts.tile([P, K_TILES, PAIRS * SIDE], F32)
         k_strips = {s: consts.tile([P, PAIRS, K_TILES, s], F32, name="k_strips%d" % s) for s in (8, 6)}
-        k_accs, relus, v_accs, v_cells, value_acc = {}, {}, {}, {}, {}
+        k_accs, relus, both_rows, two_cols, v_accs, v_cells, value_acc = {}, {}, {}, {}, {}, {}, {}
 
         def where(u):
             q, j = divmod(u, CHUNK_UNITS)
@@ -286,21 +282,21 @@ def tile_afnb_pa_t_kernel(
                     scale=gain[:, m : m + 1],
                 )
 
-        def value_matmuls(u, i_r):
+        def value_matmuls(u, i_r, g):
             q, unit = where(u)
-            if i_r == 0:
+            if i_r == UPPER and g == 0:
                 v_accs[u] = v_psum.tile([P, CV], F32, name="v_acc")
-            for i in range(CELL_W * i_r, CELL_W * (i_r + 1)):
-                for g in range(GROUPS):
-                    nc.tensor.matmul_mx(
-                        out=v_accs[u][:],
-                        lhsT=codes[:, g, q, i, unit].bitcast(FP8X4),
-                        lhsT_scale=x_scales[:, g, q, i, unit],
-                        rhs=wv_w[:, g, :].bitcast(FP4X4),
-                        rhs_scale=wv_s[:, g, :],
-                        start=(i == 0 and g == 0),
-                        stop=(i == PLANES - 1 and g == GROUPS - 1),
-                    )
+            for i_c in range(CELL_W):
+                i = CELL_W * i_r + i_c
+                nc.tensor.matmul_mx(
+                    out=v_accs[u][:],
+                    lhsT=codes[:, g, q, i, unit].bitcast(FP8X4),
+                    lhsT_scale=x_scales[:, g, q, i, unit],
+                    rhs=wv_w[:, g, :].bitcast(FP4X4),
+                    rhs_scale=wv_s[:, g, :],
+                    start=(i_r == UPPER and g == 0 and i_c == 0),
+                    stop=(i_r == LOWER and g == GROUPS - 1 and i_c == CELL_W - 1),
+                )
 
         def value_copy(u):
             v_cells[u] = work.tile([P, CV], F32, name="v_cells")
@@ -312,13 +308,29 @@ def tile_afnb_pa_t_kernel(
                 if 0 <= n < UNITS_OF_BATCH:
                     if n == 0:
                         value_acc[b] = value_psum.tile([P, CV], F32, name="value_acc")
+                        nc.tensor.matmul(out=value_acc[b][:], lhsT=ones[:], rhs=bv_row[:], start=True, stop=False)
                     nc.tensor.matmul(
                         out=value_acc[b][:],
                         lhsT=pool_w[:, UNITS_OF_BATCH * b + n, :],
                         rhs=v_cells[u][:],
-                        start=(n == 0),
+                        start=False,
                         stop=(n == UNITS_OF_BATCH - 1),
                     )
+
+        def add_rows(u):
+            both_rows[u] = work.tile([P, K_TILES, CELL_W, UNIT], F32, name="both_rows")
+            nc.vector.tensor_add(
+                out=both_rows[u][:], in0=relus[u][:, :, 0:CELL_W, :], in1=relus[u][:, :, CELL_W:PLANES, :]
+            )
+
+        def add_two_columns(u):
+            two_cols[u] = work.tile([P, K_TILES, UNIT], F32, name="two_cols")
+            nc.vector.tensor_add(out=two_cols[u][:], in0=both_rows[u][:, :, 0, :], in1=both_rows[u][:, :, 1, :])
+
+        def add_third_column(u):
+            nc.vector.tensor_add(
+                out=k_cells[:, :, UNIT * u : UNIT * (u + 1)], in0=two_cols[u][:], in1=both_rows[u][:, :, 2, :]
+            )
 
         def key_strips(u):
             first, last = UNIT * u // SIDE, UNIT * (u + 1) // SIDE
@@ -334,7 +346,7 @@ def tile_afnb_pa_t_kernel(
 
         def finish_value(b):
             value_sb = work.tile([P, CV], F32, name="value_sb")
-            nc.vector.tensor_add(out=value_sb[:], in0=value_acc[b][:], in1=bv_all[:])
+            nc.scalar.copy(out=value_sb[:], in_=value_acc[b][:])
             nc.sync.dma_start(out=out_0[b], in_=value_sb[0:LOCATIONS, :])
 
         def finish_key(b):
@@ -383,42 +395,39 @@ def tile_afnb_pa_t_kernel(
                 regroup(n, 0)
             if n == 0:
                 standard_deviation()
+            if before_last:
+                add_rows(n - 2)
             if new:
+                quantise(n, UPPER, 0)
+                value_matmuls(n, UPPER, 0)
                 regroup(n, 1)
-            if n == 0:
-                finish_small_vectors()
             if last:
                 key_relu(n - 1, LOWER)
                 value_copy(n - 1)
+            if before_last:
+                add_two_columns(n - 2)
             if new:
-                quantise(n, UPPER, 0)
                 quantise(n, UPPER, 1)
                 key_matmuls(n, UPPER)
+                value_matmuls(n, UPPER, 1)
+            if n == 0:
+                finish_small_vectors()
+            if new:
                 key_relu(n, UPPER)
-                value_matmuls(n, UPPER)
             if last:
                 value_pool(n - 1)
             if before_last:
-                relu = relus[n - 2]
-                both_rows = work.tile([P, K_TILES, CELL_W, UNIT], F32, name="both_rows")
-                nc.vector.tensor_add(
-                    out=both_rows[:], in0=relu[:, :, 0:CELL_W, :], in1=relu[:, :, CELL_W:PLANES, :]
-                )
+                add_third_column(n - 2)
             if new:
                 quantise(n, LOWER, 0)
+                value_matmuls(n, LOWER, 0)
             if before_last:
-                two_cols = work.tile([P, K_TILES, UNIT], F32, name="two_cols")
-                nc.vector.tensor_add(out=two_cols[:], in0=both_rows[:, :, 0, :], in1=both_rows[:, :, 1, :])
+                key_strips(n - 2)
             if new:
                 quantise(n, LOWER, 1)
                 key_matmuls(n, LOWER)
-                value_matmuls(n, LOWER)
-            if before_last:
-                nc.vector.tensor_add(
-                    out=k_cells[:, :, UNIT * (n - 2) : UNIT * (n - 1)], in0=two_cols[:], in1=both_rows[:, :, 2, :]
-                )
-                key_strips(n - 2)
-                q, j = divmod(n - 2, CHUNK_UNITS)
-                if j == CHUNK_UNITS - 1 and q >= 1:
-                    finish_value(q - 1)
-                    finish_key(q - 1)
+                value_matmuls(n, LOWER, 1)
+            if before_last and n - 2 in (2 * CHUNK_UNITS - 1, 3 * CHUNK_UNITS - 1):
+                b = (n - 2) // CHUNK_UNITS - 1
+                finish_value(b)
+                finish_key(b)

@@ -41,6 +41,7 @@ MAX_PAIRS = 6
 K_TILES = CK // P
 LOOKAHEAD = 2
 UPPER, LOWER = 0, 1
+PERIOD = 3
 
 FLOPS = 2 * (CK + CV) * CL * B * H * W
 
@@ -59,67 +60,106 @@ def load_weight(nc, words, scales, words_sb, scales_sb):
         )
 
 
-def build_pool_weights(nc, pool, pool_w):
+def cell_tables(nc, pool):
     edges_r, edges_c = PAIRS + 1, SIDE + 1
-    index_i = pool.tile([P, N_UNITS + edges_r + edges_c], I32)
-    nc.gpsimd.iota(index_i[:, 0:N_UNITS], pattern=[[UNIT, N_UNITS]], base=0, channel_multiplier=1)
+    start = UNIT % SIDE
+    most_rows = (P - 1 + start * (PERIOD - 1)) // SIDE
+    shifted = pool.tile([P, 2, PERIOD], F32)
     nc.gpsimd.iota(
-        index_i[:, N_UNITS : N_UNITS + edges_r], pattern=[[SIDE, edges_r]], base=0, channel_multiplier=0
+        shifted[:], pattern=[[0, 2], [start, PERIOD]], base=0, channel_multiplier=1,
+        allow_small_or_imprecise_dtypes=True,
     )
-    nc.gpsimd.iota(index_i[:, N_UNITS + edges_r :], pattern=[[1, edges_c]], base=0, channel_multiplier=0)
-    index = pool.tile([P, N_UNITS + edges_r + edges_c], F32)
-    nc.vector.tensor_copy(out=index[:], in_=index_i[:])
-    cell = index[:, 0:N_UNITS]
-    row_start = index[:, N_UNITS : N_UNITS + edges_r]
-    col_edge = index[:, N_UNITS + edges_r :]
-
+    passed = pool.tile([P, 2, PERIOD, most_rows], F32)
+    nc.gpsimd.memset(passed[:], 1.0)
+    nc.gpsimd.affine_select(
+        out=passed[:], in_=passed[:], pattern=[[0, 2], [start, PERIOD], [-SIDE, most_rows]],
+        compare_op=ALU.is_ge, fill=0.0, base=-SIDE, channel_multiplier=1,
+    )
+    col_edge = pool.tile([P, edges_c], F32)
+    nc.gpsimd.iota(
+        col_edge[:], pattern=[[1, edges_c]], base=0, channel_multiplier=0, allow_small_or_imprecise_dtypes=True
+    )
     reached_r = pool.tile([P, N_UNITS, edges_r], F32)
-    nc.vector.tensor_tensor(
-        out=reached_r[:],
-        in0=cell.unsqueeze(2).to_broadcast([P, N_UNITS, edges_r]),
-        in1=row_start.unsqueeze(1).to_broadcast([P, N_UNITS, edges_r]),
-        op=ALU.is_ge,
+    nc.gpsimd.memset(reached_r[:], 1.0)
+    nc.gpsimd.affine_select(
+        out=reached_r[:], in_=reached_r[:], pattern=[[UNIT, N_UNITS], [-SIDE, edges_r]],
+        compare_op=ALU.is_ge, fill=0.0, base=0, channel_multiplier=1,
     )
-    row = pool.tile([P, N_UNITS], F32)
-    nc.vector.tensor_reduce(out=row[:], in_=reached_r[:, :, 1:edges_r], axis=AXIS.X, op=ALU.add)
-    col = pool.tile([P, N_UNITS], F32)
-    nc.vector.scalar_tensor_tensor(
-        out=col[:], in0=row[:], scalar=-float(SIDE), in1=cell, op0=ALU.mult, op1=ALU.add
-    )
-    reached_c = pool.tile([P, N_UNITS, edges_c], F32)
-    nc.vector.tensor_tensor(
-        out=reached_c[:],
-        in0=col[:].unsqueeze(2).to_broadcast([P, N_UNITS, edges_c]),
-        in1=col_edge.unsqueeze(1).to_broadcast([P, N_UNITS, edges_c]),
-        op=ALU.is_ge,
-    )
+    return shifted, passed, col_edge, reached_r
 
+
+def pool_weight_steps(nc, pool, tables, pool_w):
+    shifted, passed, col_edge, reached_r = tables
+    edges_c = SIDE + 1
+    n_cols = 2 * PERIOD
+    row_hot, col_hot = {}, {}
+
+    def make_row_hot(s):
+        step = SIDE // s
+        row_hot[s] = pool.tile([P, N_UNITS, B * s], F32, name="row_hot%d" % s)
+        nc.vector.tensor_sub(
+            out=row_hot[s][:], in0=reached_r[:, :, 0:PAIRS:step], in1=reached_r[:, :, step : PAIRS + 1 : step]
+        )
+
+    rows_on = pool.tile([P, n_cols], F32)
+    nc.vector.tensor_reduce(
+        out=rows_on[:], in_=passed[:].rearrange("p a n i -> p (a n) i"), axis=AXIS.X, op=ALU.add
+    )
     nc.vector.memset(pool_w[:, :, LOCATIONS:P], 0.0)
-    offset = 0
+    col = pool.tile([P, n_cols], F32)
+    nc.vector.scalar_tensor_tensor(
+        out=col[:], in0=rows_on[:], scalar=-float(SIDE), in1=shifted[:].rearrange("p a n -> p (a n)"),
+        op0=ALU.mult, op1=ALU.add,
+    )
+    reached_c = pool.tile([P, n_cols, edges_c], F32)
+    before_c = pool.tile([P, n_cols, edges_c], F32)
+    for steps_c, op in ((reached_c, ALU.is_ge), (before_c, ALU.is_lt)):
+        nc.vector.tensor_tensor(
+            out=steps_c[:],
+            in0=col[:].unsqueeze(2).to_broadcast([P, n_cols, edges_c]),
+            in1=col_edge[:].unsqueeze(1).to_broadcast([P, n_cols, edges_c]),
+            op=op,
+        )
     for s in GRIDS:
         step = SIDE // s
-        row_hot = pool.tile([P, N_UNITS, B * s], F32, name="row_hot%d" % s)
-        nc.vector.tensor_sub(
-            out=row_hot[:], in0=reached_r[:, :, 0:PAIRS:step], in1=reached_r[:, :, step : PAIRS + 1 : step]
+        col_hot[s] = pool.tile([P, n_cols, s], F32, name="col_hot%d" % s)
+        nc.vector.scalar_tensor_tensor(
+            out=col_hot[s][:],
+            in0=reached_c[:, :, 0:SIDE:step],
+            scalar=1.0 / ((H // s) * (W // s)),
+            in1=before_c[:, :, step : SIDE + 1 : step],
+            op0=ALU.mult,
+            op1=ALU.mult,
         )
-        col_hot = pool.tile([P, N_UNITS, s], F32, name="col_hot%d" % s)
-        nc.vector.tensor_sub(
-            out=col_hot[:], in0=reached_c[:, :, 0:SIDE:step], in1=reached_c[:, :, step : SIDE + 1 : step]
+    for s in GRIDS:
+        make_row_hot(s)
+
+    def product(s, b, offset):
+        first = (UNITS_OF_BATCH - 1) * b
+        shape = [P, UNITS_OF_BATCH, s, s]
+        nc.vector.tensor_tensor(
+            out=pool_w[:, UNITS_OF_BATCH * b : UNITS_OF_BATCH * (b + 1), offset : offset + s * s].rearrange(
+                "p u (i j) -> p u i j", j=s
+            ),
+            in0=row_hot[s][:, first : first + UNITS_OF_BATCH, s * b : s * (b + 1)].unsqueeze(3).to_broadcast(shape),
+            in1=col_hot[s][:, first % PERIOD : first % PERIOD + UNITS_OF_BATCH, :].unsqueeze(2).to_broadcast(shape),
+            op=ALU.mult,
         )
-        col_share = pool.tile([P, N_UNITS, s], F32, name="col_share%d" % s)
-        nc.vector.tensor_scalar_mul(out=col_share[:], in0=col_hot[:], scalar1=1.0 / ((H // s) * (W // s)))
+
+    steps = []
+    offset = 0
+    for s in GRIDS:
         for b in range(B):
-            units = slice((UNITS_OF_BATCH - 1) * b, (UNITS_OF_BATCH - 1) * b + UNITS_OF_BATCH)
-            shape = [P, UNITS_OF_BATCH, s, s]
-            nc.vector.tensor_tensor(
-                out=pool_w[:, UNITS_OF_BATCH * b : UNITS_OF_BATCH * (b + 1), offset : offset + s * s].rearrange(
-                    "p u (i j) -> p u i j", j=s
-                ),
-                in0=row_hot[:, units, s * b : s * (b + 1)].unsqueeze(3).to_broadcast(shape),
-                in1=col_share[:, units, :].unsqueeze(2).to_broadcast(shape),
-                op=ALU.mult,
-            )
+            steps.append(lambda s=s, b=b, offset=offset: product(s, b, offset))
         offset += s * s
+    return steps
+
+
+def weave(first, second):
+    for n in range(max(len(first), len(second))):
+        for calls in (first, second):
+            if n < len(calls):
+                calls[n]()
 
 
 def tile_afnb_pa_t_kernel(
@@ -140,55 +180,57 @@ def tile_afnb_pa_t_kernel(
             "b (g p t) (r i) w -> b g p t r (i w)", g=GROUPS, p=P, t=PACK, i=CELL_H
         )
 
-        def load(u):
+        def load_group(u, g):
             q, j = divmod(u, CHUNK_UNITS)
             first = CHUNK_PAIRS * q + first_pair(j)
             last = CHUNK_PAIRS * q + first_pair(j + 1)
-            tiles = []
-            for g in range(GROUPS):
-                raw = raw_pool.tile([P, PACK, MAX_PAIRS, PAIR_PX], BF16, name="raw%d" % g)
-                for b in range(B):
-                    lo, hi = max(first, SIDE * b), min(last, SIDE * (b + 1))
-                    if lo < hi:
-                        nc.sync.dma_start(
-                            out=raw[:, :, lo - first : hi - first, :],
-                            in_=x_rows[b, g, :, :, lo - SIDE * b : hi - SIDE * b, :],
-                        )
-                tiles.append(raw)
-            return tiles
+            raw = raw_pool.tile([P, PACK, MAX_PAIRS, PAIR_PX], BF16, name="raw%d" % g)
+            for b in range(B):
+                lo, hi = max(first, SIDE * b), min(last, SIDE * (b + 1))
+                if lo < hi:
+                    nc.sync.dma_start(
+                        out=raw[:, :, lo - first : hi - first, :],
+                        in_=x_rows[b, g, :, :, lo - SIDE * b : hi - SIDE * b, :],
+                    )
+            return raw
 
-        raws = {0: load(0)}
+        def load(u):
+            return [load_group(u, g) for g in range(GROUPS)]
 
         wk_w = consts.tile([P, GROUPS, 2 * CK], U8, align_bytes=64)
         wv_w = consts.tile([P, GROUPS, 2 * CV], U8, align_bytes=64)
         wk_s = consts.tile([P, GROUPS, CK], U8, align_bytes=64)
         wv_s = consts.tile([P, GROUPS, CV], U8, align_bytes=64)
-        nc.vector.memset(wk_s[:].bitcast(I32), 0)
-        nc.vector.memset(wv_s[:].bitcast(I32), 0)
-        load_weight(nc, wk_words, wk_scales, wk_w, wk_s)
-        load_weight(nc, wv_words, wv_scales, wv_w, wv_s)
-        for u in range(1, LOOKAHEAD):
-            raws[u] = load(u)
-
         vectors = (bk, gk, bek, mk, vk)
         rows_sb = consts.tile([P, P], BF16)
-        nc.vector.memset(rows_sb[:], 0.0)
         bv_row = consts.tile([P, CV], BF16)
-        nc.vector.memset(bv_row[:], 0.0)
         ones = consts.tile([P, P], BF16)
+        nc.vector.memset(wv_s[:].bitcast(I32), 0)
+        nc.vector.memset(rows_sb[:], 0.0)
+        nc.vector.memset(wk_s[:].bitcast(I32), 0)
+        nc.vector.memset(bv_row[:], 0.0)
         nc.vector.memset(ones[:], 1.0)
+
+        first_raw = [load_group(0, 0)]
+        load_weight(nc, wv_words, wv_scales, wv_w, wv_s)
         for n, vector in enumerate(vectors):
-            nc.scalar.dma_start(
+            nc.sync.dma_start(
                 out=rows_sb[K_TILES * n : K_TILES * (n + 1), :], in_=vector.rearrange("(m c) -> m c", m=K_TILES)
             )
-        nc.scalar.dma_start(out=bv_row[0:1, :], in_=bv.rearrange("(o c) -> o c", o=1))
+        first_raw.append(load_group(0, 1))
+        load_weight(nc, wk_words, wk_scales, wk_w, wk_s)
+        nc.sync.dma_start(out=bv_row[0:1, :], in_=bv.rearrange("(o c) -> o c", o=1))
+        raws = {0: first_raw}
+        for u in range(1, LOOKAHEAD):
+            raws[u] = load(u)
         warm = consts.tile([P, 1], F32)
         nc.scalar.sqrt(out=warm[:], in_=ones[:, 0:1])
 
         pool_w = consts.tile([P, B * UNITS_OF_BATCH, P], F32)
-        build_pool_weights(nc, consts, pool_w)
+        tables = cell_tables(nc, consts)
         identity = consts.tile([P, P], BF16)
         make_identity(nc, identity[:])
+        pool_products = pool_weight_steps(nc, consts, tables, pool_w)
 
         cols_ps = k_psum.tile([P, P], BF16, name="cols_ps", tag="k_acc")
         nc.tensor.transpose(out=cols_ps[:], in_=rows_sb[:], identity=identity[:])
@@ -196,25 +238,26 @@ def tile_afnb_pa_t_kernel(
         std = consts.tile([P, K_TILES], F32)
         gain = consts.tile([P, K_TILES], F32)
         shift = consts.tile([P, K_TILES], F32)
+        cols = consts.tile([P, len(vectors), K_TILES], F32)
+        inv_std = consts.tile([P, K_TILES], F32)
+        centred = consts.tile([P, K_TILES], F32)
+        scaled = consts.tile([P, K_TILES], F32)
+        bk_c, gk_c, bek_c, mk_c = (cols[:, n, :] for n in range(4))
 
         def standard_deviation():
             vk_at = K_TILES * (len(vectors) - 1)
             nc.scalar.activation(out=std[:], in_=cols_ps[:, vk_at : vk_at + K_TILES], func=ACT.Sqrt, bias=EPS)
 
-        def finish_small_vectors():
-            cols = consts.tile([P, len(vectors), K_TILES], F32)
-            nc.vector.tensor_copy(
+        small_vector_steps = [
+            lambda: nc.vector.tensor_copy(
                 out=cols[:].rearrange("p n m -> p (n m)"), in_=cols_ps[:, 0 : len(vectors) * K_TILES]
-            )
-            bk_c, gk_c, bek_c, mk_c = (cols[:, n, :] for n in range(4))
-            inv_std = consts.tile([P, K_TILES], F32)
-            nc.vector.reciprocal(out=inv_std[:], in_=std[:])
-            centred = consts.tile([P, K_TILES], F32)
-            nc.vector.tensor_sub(out=centred[:], in0=bk_c, in1=mk_c)
-            nc.vector.tensor_mul(out=gain[:], in0=gk_c, in1=inv_std[:])
-            scaled = consts.tile([P, K_TILES], F32)
-            nc.vector.tensor_mul(out=scaled[:], in0=centred[:], in1=gain[:])
-            nc.vector.tensor_add(out=shift[:], in0=scaled[:], in1=bek_c)
+            ),
+            lambda: nc.vector.reciprocal(out=inv_std[:], in_=std[:]),
+            lambda: nc.vector.tensor_sub(out=centred[:], in0=bk_c, in1=mk_c),
+            lambda: nc.vector.tensor_mul(out=gain[:], in0=gk_c, in1=inv_std[:]),
+            lambda: nc.vector.tensor_mul(out=scaled[:], in0=centred[:], in1=gain[:]),
+            lambda: nc.vector.tensor_add(out=shift[:], in0=scaled[:], in1=bek_c),
+        ]
 
         grouped = [
             consts.tile([P, PLANES, CHUNK_CELLS, PACK], BF16, name="grouped%d" % g, align_bytes=64)
@@ -393,13 +436,15 @@ def tile_afnb_pa_t_kernel(
                 raws[n + LOOKAHEAD] = load(n + LOOKAHEAD)
             if new:
                 regroup(n, 0)
-            if n == 0:
-                standard_deviation()
             if before_last:
                 add_rows(n - 2)
             if new:
                 quantise(n, UPPER, 0)
                 value_matmuls(n, UPPER, 0)
+            if n == 0:
+                standard_deviation()
+                weave(pool_products[0:6], small_vector_steps)
+            if new:
                 regroup(n, 1)
             if last:
                 key_relu(n - 1, LOWER)
@@ -411,7 +456,7 @@ def tile_afnb_pa_t_kernel(
                 key_matmuls(n, UPPER)
                 value_matmuls(n, UPPER, 1)
             if n == 0:
-                finish_small_vectors()
+                weave(pool_products[6:8], [])
             if new:
                 key_relu(n, UPPER)
             if last:

@@ -41,6 +41,8 @@ MAX_PAIRS = 6
 K_TILES = CK // P
 LOOKAHEAD = 2
 UPPER, LOWER = 0, 1
+EARLY, LATE = 0, 1
+EARLY_PLANES = 2
 PERIOD = 3
 
 FLOPS = 2 * (CK + CV) * CL * B * H * W
@@ -263,8 +265,8 @@ def tile_afnb_pa_t_kernel(
             consts.tile([P, PLANES, CHUNK_CELLS, PACK], BF16, name="grouped%d" % g, align_bytes=64)
             for g in range(GROUPS)
         ]
-        codes = consts.tile([P, GROUPS, N_CHUNKS, PLANES, CHUNK_CELLS], U32, align_bytes=64)
-        x_scales = consts.tile([P, GROUPS, N_CHUNKS, PLANES, CHUNK_CELLS], U8, align_bytes=64)
+        codes = consts.tile([P, GROUPS, N_UNITS, PLANES, UNIT], U32, align_bytes=64)
+        x_scales = consts.tile([P, GROUPS, N_UNITS, PLANES, UNIT], U8, align_bytes=64)
         k_cells = consts.tile([P, K_TILES, PAIRS * SIDE], F32)
         k_strips = {s: consts.tile([P, PAIRS, K_TILES, s], F32, name="k_strips%d" % s) for s in (8, 6)}
         k_accs, relus, both_rows, two_cols, v_accs, v_cells, value_acc = {}, {}, {}, {}, {}, {}, {}
@@ -290,51 +292,59 @@ def tile_afnb_pa_t_kernel(
             q, unit = where(u)
             for i in range(CELL_W * i_r, CELL_W * (i_r + 1)):
                 nc.vector.quantize_mx(
-                    out=codes[:, g, q, i, unit].bitcast(FP8X4),
-                    scales=x_scales[:, g, q, i, unit],
+                    out=codes[:, g, u, i, :].bitcast(FP8X4),
+                    scales=x_scales[:, g, u, i, :],
                     in_=grouped[g][:, i, unit, :].rearrange("p c t -> p (c t)"),
                 )
 
-        def key_matmuls(u, i_r):
-            q, unit = where(u)
-            for m in range(K_TILES):
-                k_acc = k_psum.tile([P, CELL_W, UNIT], F32, name="k_acc")
-                for i_c in range(CELL_W):
-                    i = CELL_W * i_r + i_c
-                    for g in range(GROUPS):
-                        nc.tensor.matmul_mx(
-                            out=k_acc[:, i_c, :],
-                            lhsT=wk_w[:, g, 2 * P * m : 2 * P * (m + 1)].bitcast(FP4X4),
-                            lhsT_scale=wk_s[:, g, P * m : P * (m + 1)],
-                            rhs=codes[:, g, q, i, unit].bitcast(FP8X4),
-                            rhs_scale=x_scales[:, g, q, i, unit],
-                            start=(g == 0),
-                            stop=(g == GROUPS - 1),
-                        )
-                k_accs[u, i_r, m] = k_acc
+        def key_pass(out, u, m, g, planes):
+            nc.tensor.matmul_mx(
+                out=out,
+                lhsT=wk_w[:, g, 2 * P * m : 2 * P * (m + 1)].bitcast(FP4X4),
+                lhsT_scale=wk_s[:, g, P * m : P * (m + 1)],
+                rhs=codes[:, g, u, planes, :].rearrange("p k c -> p (k c)").bitcast(FP8X4),
+                rhs_scale=x_scales[:, g, u, planes, :].rearrange("p k c -> p (k c)"),
+                start=(g == 0),
+                stop=(g == GROUPS - 1),
+            )
 
-        def key_relu(u, i_r):
-            if i_r == 0:
+        def key_matmuls(u, step):
+            if step == EARLY:
+                k_acc = k_psum.tile([P, K_TILES, EARLY_PLANES, UNIT], F32, name="k_acc")
+                for m in range(K_TILES):
+                    for i in range(EARLY_PLANES):
+                        for g in range(GROUPS):
+                            key_pass(k_acc[:, m, i, :], u, m, g, slice(i, i + 1))
+                    k_accs[u, step, m] = k_acc[:, m, :, :]
+            else:
+                for m in range(K_TILES):
+                    k_acc = k_psum.tile([P, PLANES - EARLY_PLANES, UNIT], F32, name="k_acc")
+                    for g in range(GROUPS):
+                        key_pass(k_acc[:].rearrange("p k c -> p (k c)"), u, m, g, slice(EARLY_PLANES, PLANES))
+                    k_accs[u, step, m] = k_acc[:]
+
+        def key_relu(u, step):
+            if step == EARLY:
                 relus[u] = relu_pool.tile([P, K_TILES, PLANES, UNIT], F32, name="relu")
+            planes = slice(0, EARLY_PLANES) if step == EARLY else slice(EARLY_PLANES, PLANES)
             for m in range(K_TILES):
                 nc.scalar.activation(
-                    out=relus[u][:, m, CELL_W * i_r : CELL_W * (i_r + 1), :],
-                    in_=k_accs[u, i_r, m][:],
+                    out=relus[u][:, m, planes, :],
+                    in_=k_accs[u, step, m],
                     func=ACT.Relu,
                     bias=shift[:, m : m + 1],
                     scale=gain[:, m : m + 1],
                 )
 
         def value_matmuls(u, i_r, g):
-            q, unit = where(u)
             if i_r == UPPER and g == 0:
                 v_accs[u] = v_psum.tile([P, CV], F32, name="v_acc")
             for i_c in range(CELL_W):
                 i = CELL_W * i_r + i_c
                 nc.tensor.matmul_mx(
                     out=v_accs[u][:],
-                    lhsT=codes[:, g, q, i, unit].bitcast(FP8X4),
-                    lhsT_scale=x_scales[:, g, q, i, unit],
+                    lhsT=codes[:, g, u, i, :].bitcast(FP8X4),
+                    lhsT_scale=x_scales[:, g, u, i, :],
                     rhs=wv_w[:, g, :].bitcast(FP4X4),
                     rhs_scale=wv_s[:, g, :],
                     start=(i_r == UPPER and g == 0 and i_c == 0),
@@ -447,18 +457,18 @@ def tile_afnb_pa_t_kernel(
             if new:
                 regroup(n, 1)
             if last:
-                key_relu(n - 1, LOWER)
+                key_relu(n - 1, LATE)
                 value_copy(n - 1)
             if before_last:
                 add_two_columns(n - 2)
             if new:
                 quantise(n, UPPER, 1)
-                key_matmuls(n, UPPER)
+                key_matmuls(n, EARLY)
                 value_matmuls(n, UPPER, 1)
             if n == 0:
                 weave(pool_products[6:8], [])
             if new:
-                key_relu(n, UPPER)
+                key_relu(n, EARLY)
             if last:
                 value_pool(n - 1)
             if before_last:
@@ -470,7 +480,7 @@ def tile_afnb_pa_t_kernel(
                 key_strips(n - 2)
             if new:
                 quantise(n, LOWER, 1)
-                key_matmuls(n, LOWER)
+                key_matmuls(n, LATE)
                 value_matmuls(n, LOWER, 1)
             if before_last and n - 2 in (2 * CHUNK_UNITS - 1, 3 * CHUNK_UNITS - 1):
                 b = (n - 2) // CHUNK_UNITS - 1

@@ -43,6 +43,7 @@ LOOKAHEAD = 2
 UPPER, LOWER = 0, 1
 EARLY, LATE = 0, 1
 EARLY_PLANES = 2
+S_CELLS = 20
 PERIOD = 3
 
 FLOPS = 2 * (CK + CV) * CL * B * H * W
@@ -278,14 +279,19 @@ def tile_afnb_pa_t_kernel(
         def regroup(u, g):
             j = u % CHUNK_UNITS
             lo, hi = first_pair(j), first_pair(j + 1)
-            for i_r, copy in enumerate((nc.vector.tensor_copy, nc.scalar.copy)):
+            shares = (
+                (nc.vector.tensor_copy, UPPER, 0, SIDE),
+                (nc.scalar.copy, LOWER, 0, S_CELLS),
+                (nc.vector.tensor_copy, LOWER, S_CELLS, SIDE),
+            )
+            for copy, i_r, c0, c1 in shares:
                 copy(
                     out=grouped[g][:, CELL_W * i_r : CELL_W * (i_r + 1), SIDE * lo : SIDE * hi, :].rearrange(
                         "p k (r c) t -> p r c t k", c=SIDE
-                    ),
+                    )[:, :, c0:c1, :, :],
                     in_=raws[u][g][:, :, 0 : hi - lo, W * i_r : W * (i_r + 1)].rearrange(
                         "p t r (c k) -> p r c t k", k=CELL_W
-                    ),
+                    )[:, :, c0:c1, :, :],
                 )
 
         def quantise(u, i_r, g):

@@ -220,9 +220,9 @@ def tile_afnb_pa_t_kernel(
             nc.sync.dma_start(
                 out=rows_sb[K_TILES * n : K_TILES * (n + 1), :], in_=vector.rearrange("(m c) -> m c", m=K_TILES)
             )
+        nc.sync.dma_start(out=bv_row[0:1, :], in_=bv.rearrange("(o c) -> o c", o=1))
         first_raw.append(load_group(0, 1))
         load_weight(nc, wk_words, wk_scales, wk_w, wk_s)
-        nc.sync.dma_start(out=bv_row[0:1, :], in_=bv.rearrange("(o c) -> o c", o=1))
         raws = {0: first_raw}
         for u in range(1, LOOKAHEAD):
             raws[u] = load(u)
@@ -361,13 +361,15 @@ def tile_afnb_pa_t_kernel(
             v_cells[u] = work.tile([P, CV], F32, name="v_cells")
             nc.scalar.copy(out=v_cells[u][:], in_=v_accs[u][:])
 
+        def value_bias():
+            for b in range(B):
+                value_acc[b] = value_psum.tile([P, CV], F32, name="value_acc")
+                nc.tensor.matmul(out=value_acc[b][:], lhsT=ones[:], rhs=bv_row[:], start=True, stop=False)
+
         def value_pool(u):
             for b in range(B):
                 n = u - (UNITS_OF_BATCH - 1) * b
                 if 0 <= n < UNITS_OF_BATCH:
-                    if n == 0:
-                        value_acc[b] = value_psum.tile([P, CV], F32, name="value_acc")
-                        nc.tensor.matmul(out=value_acc[b][:], lhsT=ones[:], rhs=bv_row[:], start=True, stop=False)
                     nc.tensor.matmul(
                         out=value_acc[b][:],
                         lhsT=pool_w[:, UNITS_OF_BATCH * b + n, :],
@@ -409,45 +411,48 @@ def tile_afnb_pa_t_kernel(
             nc.sync.dma_start(out=out_0[b], in_=value_sb[0:LOCATIONS, :])
 
         def finish_key(b):
-            sums = {s: work.tile([P, s, K_TILES, s], F32, name="sums%d" % s) for s in GRIDS}
-            for s, strips in k_strips.items():
+            sums = {s: work.tile([P, K_TILES, s, s], F32, name="sums%d" % s) for s in GRIDS}
+            key_sb = work.tile([P, K_TILES, LOCATIONS], F32, name="key_sb")
+            offsets = {s: sum(c * c for c in GRIDS[: GRIDS.index(s)]) for s in GRIDS}
+
+            def from_strips(s):
                 nc.vector.tensor_reduce(
-                    out=sums[s][:].rearrange("p i m j -> p i (m j)"),
-                    in_=strips[:, SIDE * b : SIDE * (b + 1), :, :].rearrange(
-                        "p (i k) m j -> p i (m j) k", k=SIDE // s
+                    out=sums[s][:],
+                    in_=k_strips[s][:, SIDE * b : SIDE * (b + 1), :, :].rearrange(
+                        "p (i k) m j -> p m i j k", k=SIDE // s
                     ),
                     axis=AXIS.X,
                     op=ALU.add,
                 )
-            halves = work.tile([P, 6, K_TILES, 3], F32, name="halves")
+
+            def mean(s):
+                nc.vector.tensor_scalar_mul(
+                    out=key_sb[:, :, offsets[s] : offsets[s] + s * s],
+                    in0=sums[s][:].rearrange("p m i j -> p m (i j)"),
+                    scalar1=1.0 / ((H // s) * (W // s)),
+                )
+
+            from_strips(6)
+            from_strips(8)
             nc.vector.tensor_reduce(
-                out=halves[:], in_=sums[6][:].rearrange("p i m (j k) -> p i m j k", k=2), axis=AXIS.X, op=ALU.add
-            )
-            nc.vector.tensor_reduce(
-                out=sums[3][:].rearrange("p i m j -> p i (m j)"),
-                in_=halves[:].rearrange("p (i k) m j -> p i (m j) k", k=2),
-                axis=AXIS.X,
-                op=ALU.add,
-            )
-            nc.vector.tensor_reduce(
-                out=sums[1][:].rearrange("p i m j -> p (i m j)"),
-                in_=sums[3][:].rearrange("p i m j -> p m i j"),
+                out=sums[3][:].rearrange("p m i j -> p (m i) j"),
+                in_=sums[6][:].rearrange("p m (i a) (j c) -> p (m i) j a c", a=2, c=2),
                 axis=AXIS.XY,
                 op=ALU.add,
             )
-            key_sb = work.tile([P, K_TILES, LOCATIONS], F32, name="key_sb")
-            offset = 0
-            for s in GRIDS:
-                nc.vector.tensor_scalar_mul(
-                    out=key_sb[:, :, offset : offset + s * s].rearrange("p m (i j) -> p m i j", j=s),
-                    in0=sums[s][:].rearrange("p i m j -> p m i j"),
-                    scalar1=1.0 / ((H // s) * (W // s)),
-                )
-                offset += s * s
+            nc.vector.tensor_reduce(
+                out=sums[1][:].rearrange("p m i j -> p (m i j)"),
+                in_=sums[6][:].rearrange("p m i j -> p m (i j)"),
+                axis=AXIS.X,
+                op=ALU.add,
+            )
+            for s in (6, 8, 3, 1):
+                mean(s)
             nc.sync.dma_start(out=out_1[b].rearrange("(m c) l -> c m l", m=K_TILES), in_=key_sb[:])
 
         for n in range(N_UNITS + 2):
             new, last, before_last = n < N_UNITS, 1 <= n <= N_UNITS, n >= 2
+            closing = n == N_UNITS - 1
             if n + LOOKAHEAD < N_UNITS:
                 raws[n + LOOKAHEAD] = load(n + LOOKAHEAD)
             if new:
@@ -458,6 +463,7 @@ def tile_afnb_pa_t_kernel(
                 quantise(n, UPPER, 0)
                 value_matmuls(n, UPPER, 0)
             if n == 0:
+                value_bias()
                 standard_deviation()
                 weave(pool_products[0:6], small_vector_steps)
             if new:
@@ -475,19 +481,25 @@ def tile_afnb_pa_t_kernel(
                 weave(pool_products[6:8], [])
             if new:
                 key_relu(n, EARLY)
-            if last:
+            if last and not closing:
                 value_pool(n - 1)
             if before_last:
                 add_third_column(n - 2)
             if new:
                 quantise(n, LOWER, 0)
+            if new and not closing:
                 value_matmuls(n, LOWER, 0)
             if before_last:
                 key_strips(n - 2)
             if new:
                 quantise(n, LOWER, 1)
                 key_matmuls(n, LATE)
+            if closing:
+                value_matmuls(n, LOWER, 0)
+            if new:
                 value_matmuls(n, LOWER, 1)
+            if closing:
+                value_pool(n - 1)
             if before_last and n - 2 in (2 * CHUNK_UNITS - 1, 3 * CHUNK_UNITS - 1):
                 b = (n - 2) // CHUNK_UNITS - 1
                 finish_value(b)

@@ -39,7 +39,7 @@ UNITS_OF_BATCH = 5
 MAX_PAIRS = 6
 
 K_TILES = CK // P
-LOOKAHEAD = 2
+LOOKAHEAD = 3
 UPPER, LOWER = 0, 1
 EARLY, LATE = 0, 1
 EARLY_PLANES = 2

@@ -44,6 +44,7 @@ UPPER, LOWER = 0, 1
 EARLY, LATE = 0, 1
 EARLY_PLANES = 2
 S_CELLS = 20
+STRIPS_AFTER = {2: 3, 5: 3, 7: 2, 8: 1}
 PERIOD = 3
 
 FLOPS = 2 * (CK + CV) * CL * B * H * W
@@ -251,16 +252,16 @@ def tile_afnb_pa_t_kernel(
             vk_at = K_TILES * (len(vectors) - 1)
             nc.scalar.activation(out=std[:], in_=cols_ps[:, vk_at : vk_at + K_TILES], func=ACT.Sqrt, bias=EPS)
 
-        small_vector_steps = [
-            lambda: nc.vector.tensor_copy(
-                out=cols[:].rearrange("p n m -> p (n m)"), in_=cols_ps[:, 0 : len(vectors) * K_TILES]
-            ),
-            lambda: nc.vector.reciprocal(out=inv_std[:], in_=std[:]),
-            lambda: nc.vector.tensor_sub(out=centred[:], in0=bk_c, in1=mk_c),
-            lambda: nc.vector.tensor_mul(out=gain[:], in0=gk_c, in1=inv_std[:]),
-            lambda: nc.vector.tensor_mul(out=scaled[:], in0=centred[:], in1=gain[:]),
-            lambda: nc.vector.tensor_add(out=shift[:], in0=scaled[:], in1=bek_c),
-        ]
+        def small_vectors_out():
+            nc.scalar.copy(out=cols[:].rearrange("p n m -> p (n m)"), in_=cols_ps[:, 0 : len(vectors) * K_TILES])
+            standard_deviation()
+            nc.gpsimd.tensor_sub(out=centred[:], in0=bk_c, in1=mk_c)
+
+        def gain_and_shift():
+            nc.vector.reciprocal(out=inv_std[:], in_=std[:])
+            nc.gpsimd.tensor_mul(out=gain[:], in0=gk_c, in1=inv_std[:])
+            nc.gpsimd.tensor_mul(out=scaled[:], in0=centred[:], in1=gain[:])
+            nc.gpsimd.tensor_add(out=shift[:], in0=scaled[:], in1=bek_c)
 
         grouped = [
             consts.tile([P, PLANES, CHUNK_CELLS, PACK], BF16, name="grouped%d" % g, align_bytes=64)
@@ -393,8 +394,8 @@ def tile_afnb_pa_t_kernel(
                 out=k_cells[:, :, UNIT * u : UNIT * (u + 1)], in0=two_cols[u][:], in1=both_rows[u][:, :, 2, :]
             )
 
-        def key_strips(u):
-            first, last = UNIT * u // SIDE, UNIT * (u + 1) // SIDE
+        def key_strips(u, units):
+            first, last = UNIT * u // SIDE, UNIT * (u + units) // SIDE
             for s, strips in k_strips.items():
                 nc.vector.tensor_reduce(
                     out=strips[:, first:last, :, :].rearrange("p r m j -> p m r j"),
@@ -426,10 +427,10 @@ def tile_afnb_pa_t_kernel(
                 )
 
             def mean(s):
-                nc.vector.tensor_scalar_mul(
+                nc.scalar.mul(
                     out=key_sb[:, :, offsets[s] : offsets[s] + s * s],
-                    in0=sums[s][:].rearrange("p m i j -> p m (i j)"),
-                    scalar1=1.0 / ((H // s) * (W // s)),
+                    in_=sums[s][:].rearrange("p m i j -> p m (i j)"),
+                    mul=1.0 / ((H // s) * (W // s)),
                 )
 
             from_strips(6)
@@ -464,8 +465,10 @@ def tile_afnb_pa_t_kernel(
                 value_matmuls(n, UPPER, 0)
             if n == 0:
                 value_bias()
-                standard_deviation()
-                weave(pool_products[0:6], small_vector_steps)
+                small_vectors_out()
+                weave(pool_products[0:3], [])
+                gain_and_shift()
+                weave(pool_products[3:6], [])
             if new:
                 regroup(n, 1)
             if last:
@@ -489,8 +492,8 @@ def tile_afnb_pa_t_kernel(
                 quantise(n, LOWER, 0)
             if new and not closing:
                 value_matmuls(n, LOWER, 0)
-            if before_last:
-                key_strips(n - 2)
+            if before_last and n - 2 in STRIPS_AFTER:
+                key_strips(n - 1 - STRIPS_AFTER[n - 2], STRIPS_AFTER[n - 2])
             if new:
                 quantise(n, LOWER, 1)
                 key_matmuls(n, LATE)

@@ -44,7 +44,9 @@ UPPER, LOWER = 0, 1
 EARLY, LATE = 0, 1
 EARLY_PLANES = 2
 S_CELLS = 20
-STRIPS_AFTER = {2: 3, 5: 3, 7: 2, 8: 1}
+HALVES = 2 * B
+HALF_CELLS = SIDE * SIDE // 2
+HALF_AFTER = {2: 0, 4: 1, 6: 2}
 PERIOD = 3
 
 FLOPS = 2 * (CK + CV) * CL * B * H * W
@@ -209,23 +211,23 @@ def tile_afnb_pa_t_kernel(
         rows_sb = consts.tile([P, P], BF16)
         bv_row = consts.tile([P, CV], BF16)
         ones = consts.tile([P, P], BF16)
-        nc.vector.memset(wv_s[:].bitcast(I32), 0)
         nc.vector.memset(rows_sb[:], 0.0)
+        nc.vector.memset(wv_s[:].bitcast(I32), 0)
         nc.vector.memset(wk_s[:].bitcast(I32), 0)
         nc.vector.memset(bv_row[:], 0.0)
         nc.vector.memset(ones[:], 1.0)
 
-        first_raw = [load_group(0, 0)]
-        load_weight(nc, wv_words, wv_scales, wv_w, wv_s)
         for n, vector in enumerate(vectors):
-            nc.sync.dma_start(
+            nc.scalar.dma_start(
                 out=rows_sb[K_TILES * n : K_TILES * (n + 1), :], in_=vector.rearrange("(m c) -> m c", m=K_TILES)
             )
-        nc.sync.dma_start(out=bv_row[0:1, :], in_=bv.rearrange("(o c) -> o c", o=1))
+        first_raw = [load_group(0, 0)]
+        load_weight(nc, wv_words, wv_scales, wv_w, wv_s)
         first_raw.append(load_group(0, 1))
         load_weight(nc, wk_words, wk_scales, wk_w, wk_s)
-        raws = {0: first_raw}
-        for u in range(1, LOOKAHEAD):
+        raws = {0: first_raw, 1: load(1)}
+        nc.sync.dma_start(out=bv_row[0:1, :], in_=bv.rearrange("(o c) -> o c", o=1))
+        for u in range(2, LOOKAHEAD):
             raws[u] = load(u)
         warm = consts.tile([P, 1], F32)
         nc.scalar.sqrt(out=warm[:], in_=ones[:, 0:1])
@@ -269,8 +271,10 @@ def tile_afnb_pa_t_kernel(
         ]
         codes = consts.tile([P, GROUPS, N_UNITS, PLANES, UNIT], U32, align_bytes=64)
         x_scales = consts.tile([P, GROUPS, N_UNITS, PLANES, UNIT], U8, align_bytes=64)
-        k_cells = consts.tile([P, K_TILES, PAIRS * SIDE], F32)
-        k_strips = {s: consts.tile([P, PAIRS, K_TILES, s], F32, name="k_strips%d" % s) for s in (8, 6)}
+        k_cells = [consts.tile([P, K_TILES, HALF_CELLS], F32, name="k_cells%d" % h) for h in range(HALVES)]
+        sums = [
+            {s: consts.tile([P, K_TILES, s, s], F32, name="sums%d_%d" % (s, b)) for s in GRIDS} for b in range(B)
+        ]
         k_accs, relus, both_rows, two_cols, v_accs, v_cells, value_acc = {}, {}, {}, {}, {}, {}, {}
 
         def where(u):
@@ -362,15 +366,13 @@ def tile_afnb_pa_t_kernel(
             v_cells[u] = work.tile([P, CV], F32, name="v_cells")
             nc.scalar.copy(out=v_cells[u][:], in_=v_accs[u][:])
 
-        def value_bias():
-            for b in range(B):
-                value_acc[b] = value_psum.tile([P, CV], F32, name="value_acc")
-                nc.tensor.matmul(out=value_acc[b][:], lhsT=ones[:], rhs=bv_row[:], start=True, stop=False)
-
         def value_pool(u):
             for b in range(B):
                 n = u - (UNITS_OF_BATCH - 1) * b
                 if 0 <= n < UNITS_OF_BATCH:
+                    if b not in value_acc:
+                        value_acc[b] = value_psum.tile([P, CV], F32, name="value_acc")
+                        nc.tensor.matmul(out=value_acc[b][:], lhsT=ones[:], rhs=bv_row[:], start=True, stop=False)
                     nc.tensor.matmul(
                         out=value_acc[b][:],
                         lhsT=pool_w[:, UNITS_OF_BATCH * b + n, :],
@@ -390,21 +392,59 @@ def tile_afnb_pa_t_kernel(
             nc.vector.tensor_add(out=two_cols[u][:], in0=both_rows[u][:, :, 0, :], in1=both_rows[u][:, :, 1, :])
 
         def add_third_column(u):
-            nc.vector.tensor_add(
-                out=k_cells[:, :, UNIT * u : UNIT * (u + 1)], in0=two_cols[u][:], in1=both_rows[u][:, :, 2, :]
-            )
+            for h in range(HALVES):
+                first = UNIT * u - HALF_CELLS * h
+                lo, hi = max(first, 0), min(first + UNIT, HALF_CELLS)
+                if lo < hi:
+                    cells = slice(lo - first, hi - first)
+                    nc.vector.tensor_add(
+                        out=k_cells[h][:, :, lo:hi], in0=two_cols[u][:, :, cells], in1=both_rows[u][:, :, 2, cells]
+                    )
 
-        def key_strips(u, units):
-            first, last = UNIT * u // SIDE, UNIT * (u + units) // SIDE
-            for s, strips in k_strips.items():
+        def block_sums(h):
+            b, half = divmod(h, 2)
+            pairs, rows8, rows6 = (
+                work.tile([P, K_TILES, n, SIDE], F32, name=name) for name, n in (("pairs", 4), ("rows8", 4), ("rows6", 3))
+            )
+            six = k_cells[h][:].rearrange("p m (i x c) -> p (m i) x c", x=6, c=SIDE)
+            twelve = k_cells[h][:].rearrange("p m (y c) -> p m y c", c=SIDE)
+
+            def by_six(tile):
+                return tile[:].rearrange("p m (i e) c -> p (m i) e c", e=2)
+
+            def strips(s, rows):
+                n_rows = s // 2
                 nc.vector.tensor_reduce(
-                    out=strips[:, first:last, :, :].rearrange("p r m j -> p m r j"),
-                    in_=k_cells[:, :, SIDE * first : SIDE * last].rearrange(
-                        "p m (r j k) -> p m r j k", j=s, k=SIDE // s
-                    ),
+                    out=sums[b][s][:, :, n_rows * half : n_rows * (half + 1), :],
+                    in_=rows[:].rearrange("p m i (j k) -> p m i j k", k=SIDE // s),
                     axis=AXIS.X,
                     op=ALU.add,
                 )
+
+            return [
+                lambda: nc.vector.tensor_add(out=by_six(pairs), in0=six[:, :, 0:6:4, :], in1=six[:, :, 1:6:4, :]),
+                lambda: nc.vector.tensor_add(out=by_six(rows8), in0=by_six(pairs), in1=six[:, :, 2:4, :]),
+                lambda: nc.vector.tensor_add(out=rows6[:, :, 1, :], in0=pairs[:, :, 1, :], in1=pairs[:, :, 2, :]),
+                lambda: nc.vector.tensor_add(out=rows6[:, :, 0:3:2, :], in0=rows8[:, :, 0:4:3, :], in1=twelve[:, :, 3:9:5, :]),
+                lambda: strips(8, rows8),
+                lambda: strips(6, rows6),
+            ]
+
+        def coarse_sums(b):
+            return [
+                lambda: nc.vector.tensor_reduce(
+                    out=sums[b][3][:].rearrange("p m i j -> p (m i) j"),
+                    in_=sums[b][6][:].rearrange("p m (i a) (j c) -> p (m i) j a c", a=2, c=2),
+                    axis=AXIS.XY,
+                    op=ALU.add,
+                ),
+                lambda: nc.vector.tensor_reduce(
+                    out=sums[b][1][:].rearrange("p m i j -> p (m i j)"),
+                    in_=sums[b][6][:].rearrange("p m i j -> p m (i j)"),
+                    axis=AXIS.X,
+                    op=ALU.add,
+                ),
+            ]
 
         def finish_value(b):
             value_sb = work.tile([P, CV], F32, name="value_sb")
@@ -412,98 +452,94 @@ def tile_afnb_pa_t_kernel(
             nc.sync.dma_start(out=out_0[b], in_=value_sb[0:LOCATIONS, :])
 
         def finish_key(b):
-            sums = {s: work.tile([P, K_TILES, s, s], F32, name="sums%d" % s) for s in GRIDS}
             key_sb = work.tile([P, K_TILES, LOCATIONS], F32, name="key_sb")
             offsets = {s: sum(c * c for c in GRIDS[: GRIDS.index(s)]) for s in GRIDS}
-
-            def from_strips(s):
-                nc.vector.tensor_reduce(
-                    out=sums[s][:],
-                    in_=k_strips[s][:, SIDE * b : SIDE * (b + 1), :, :].rearrange(
-                        "p (i k) m j -> p m i j k", k=SIDE // s
-                    ),
-                    axis=AXIS.X,
-                    op=ALU.add,
-                )
-
-            def mean(s):
+            for s in (6, 8, 3, 1):
                 nc.scalar.mul(
                     out=key_sb[:, :, offsets[s] : offsets[s] + s * s],
-                    in_=sums[s][:].rearrange("p m i j -> p m (i j)"),
+                    in_=sums[b][s][:].rearrange("p m i j -> p m (i j)"),
                     mul=1.0 / ((H // s) * (W // s)),
                 )
-
-            from_strips(6)
-            from_strips(8)
-            nc.vector.tensor_reduce(
-                out=sums[3][:].rearrange("p m i j -> p (m i) j"),
-                in_=sums[6][:].rearrange("p m (i a) (j c) -> p (m i) j a c", a=2, c=2),
-                axis=AXIS.XY,
-                op=ALU.add,
-            )
-            nc.vector.tensor_reduce(
-                out=sums[1][:].rearrange("p m i j -> p (m i j)"),
-                in_=sums[6][:].rearrange("p m i j -> p m (i j)"),
-                axis=AXIS.X,
-                op=ALU.add,
-            )
-            for s in (6, 8, 3, 1):
-                mean(s)
             nc.sync.dma_start(out=out_1[b].rearrange("(m c) l -> c m l", m=K_TILES), in_=key_sb[:])
 
-        for n in range(N_UNITS + 2):
-            new, last, before_last = n < N_UNITS, 1 <= n <= N_UNITS, n >= 2
+        small_vectors_out()
+
+        extra = []
+        for n in range(N_UNITS):
+            last, before_last = n >= 1, n >= 2
             closing = n == N_UNITS - 1
             if n + LOOKAHEAD < N_UNITS:
                 raws[n + LOOKAHEAD] = load(n + LOOKAHEAD)
-            if new:
-                regroup(n, 0)
+            regroup(n, 0)
             if before_last:
                 add_rows(n - 2)
-            if new:
-                quantise(n, UPPER, 0)
-                value_matmuls(n, UPPER, 0)
+            quantise(n, UPPER, 0)
+            value_matmuls(n, UPPER, 0)
             if n == 0:
-                value_bias()
-                small_vectors_out()
-                weave(pool_products[0:3], [])
                 gain_and_shift()
-                weave(pool_products[3:6], [])
-            if new:
-                regroup(n, 1)
-            if last:
+                weave(pool_products[0:4], [])
+            if n < 2:
+                quantise(n, LOWER, 0)
+                value_matmuls(n, LOWER, 0)
+            if n == 1:
+                key_relu(n - 1, EARLY)
+                key_relu(n - 1, LATE)
+                value_copy(n - 1)
+            regroup(n, 1)
+            if n > 1:
+                key_relu(n - 1, EARLY)
                 key_relu(n - 1, LATE)
                 value_copy(n - 1)
             if before_last:
                 add_two_columns(n - 2)
-            if new:
-                quantise(n, UPPER, 1)
-                key_matmuls(n, EARLY)
-                value_matmuls(n, UPPER, 1)
-            if n == 0:
-                weave(pool_products[6:8], [])
-            if new:
-                key_relu(n, EARLY)
-            if last and not closing:
-                value_pool(n - 1)
+            quantise(n, UPPER, 1)
+            key_matmuls(n, EARLY)
+            value_matmuls(n, UPPER, 1)
+            for call in extra[0:2]:
+                call()
             if before_last:
                 add_third_column(n - 2)
-            if new:
+            if n > 1:
                 quantise(n, LOWER, 0)
-            if new and not closing:
-                value_matmuls(n, LOWER, 0)
-            if before_last and n - 2 in STRIPS_AFTER:
-                key_strips(n - 1 - STRIPS_AFTER[n - 2], STRIPS_AFTER[n - 2])
-            if new:
-                quantise(n, LOWER, 1)
-                key_matmuls(n, LATE)
-            if closing:
-                value_matmuls(n, LOWER, 0)
-            if new:
-                value_matmuls(n, LOWER, 1)
-            if closing:
+                if not closing:
+                    value_matmuls(n, LOWER, 0)
+            for call in extra[2:4]:
+                call()
+            quantise(n, LOWER, 1)
+            key_matmuls(n, LATE)
+            if n == 0:
+                weave(pool_products[4:], [])
+            if last and not closing:
                 value_pool(n - 1)
-            if before_last and n - 2 in (2 * CHUNK_UNITS - 1, 3 * CHUNK_UNITS - 1):
-                b = (n - 2) // CHUNK_UNITS - 1
-                finish_value(b)
-                finish_key(b)
+            if closing:
+                value_matmuls(n, LOWER, 0)
+            value_matmuls(n, LOWER, 1)
+            for call in extra[4:]:
+                call()
+            extra = block_sums(HALF_AFTER[n - 2]) if n - 2 in HALF_AFTER else []
+            if n - 2 == 5:
+                extra = coarse_sums(0)
+        last_unit = N_UNITS - 1
+        finish_value(0)
+        value_pool(last_unit - 1)
+        key_relu(last_unit, EARLY)
+        key_relu(last_unit, LATE)
+        value_copy(last_unit)
+        value_pool(last_unit)
+        finish_key(0)
+        add_rows(last_unit - 1)
+        for call in extra[0:2]:
+            call()
+        add_two_columns(last_unit - 1)
+        for call in extra[2:4]:
+            call()
+        add_third_column(last_unit - 1)
+        for call in extra[4:]:
+            call()
+        add_rows(last_unit)
+        add_two_columns(last_unit)
+        add_third_column(last_unit)
+        for call in block_sums(HALVES - 1) + coarse_sums(1):
+            call()
+        finish_key(1)
+        finish_value(1)

@@ -381,24 +381,32 @@ def tile_afnb_pa_t_kernel(
                         stop=(n == UNITS_OF_BATCH - 1),
                     )
 
-        def add_rows(u):
-            both_rows[u] = work.tile([P, K_TILES, CELL_W, UNIT], F32, name="both_rows")
+        def add_rows(u, tiles=slice(0, K_TILES)):
+            if u not in both_rows:
+                both_rows[u] = work.tile([P, K_TILES, CELL_W, UNIT], F32, name="both_rows")
             nc.vector.tensor_add(
-                out=both_rows[u][:], in0=relus[u][:, :, 0:CELL_W, :], in1=relus[u][:, :, CELL_W:PLANES, :]
+                out=both_rows[u][:, tiles, :, :],
+                in0=relus[u][:, tiles, 0:CELL_W, :],
+                in1=relus[u][:, tiles, CELL_W:PLANES, :],
             )
 
-        def add_two_columns(u):
-            two_cols[u] = work.tile([P, K_TILES, UNIT], F32, name="two_cols")
-            nc.vector.tensor_add(out=two_cols[u][:], in0=both_rows[u][:, :, 0, :], in1=both_rows[u][:, :, 1, :])
+        def add_two_columns(u, tiles=slice(0, K_TILES)):
+            if u not in two_cols:
+                two_cols[u] = work.tile([P, K_TILES, UNIT], F32, name="two_cols")
+            nc.vector.tensor_add(
+                out=two_cols[u][:, tiles, :], in0=both_rows[u][:, tiles, 0, :], in1=both_rows[u][:, tiles, 1, :]
+            )
 
-        def add_third_column(u):
+        def add_third_column(u, tiles=slice(0, K_TILES)):
             for h in range(HALVES):
                 first = UNIT * u - HALF_CELLS * h
                 lo, hi = max(first, 0), min(first + UNIT, HALF_CELLS)
                 if lo < hi:
                     cells = slice(lo - first, hi - first)
                     nc.vector.tensor_add(
-                        out=k_cells[h][:, :, lo:hi], in0=two_cols[u][:, :, cells], in1=both_rows[u][:, :, 2, cells]
+                        out=k_cells[h][:, tiles, lo:hi],
+                        in0=two_cols[u][:, tiles, cells],
+                        in1=both_rows[u][:, tiles, 2, cells],
                     )
 
         def block_sums(h):
@@ -486,6 +494,9 @@ def tile_afnb_pa_t_kernel(
                 key_relu(n - 1, LATE)
                 value_copy(n - 1)
             regroup(n, 1)
+            if closing:
+                finish_value(0)
+                finish_key(0)
             if n > 1:
                 key_relu(n - 1, EARLY)
                 key_relu(n - 1, LATE)
@@ -517,16 +528,14 @@ def tile_afnb_pa_t_kernel(
             for call in extra[4:]:
                 call()
             extra = block_sums(HALF_AFTER[n - 2]) if n - 2 in HALF_AFTER else []
-            if n - 2 == 5:
-                extra = coarse_sums(0)
+            if n - 2 == 4:
+                extra += coarse_sums(0)
         last_unit = N_UNITS - 1
-        finish_value(0)
         value_pool(last_unit - 1)
         key_relu(last_unit, EARLY)
         key_relu(last_unit, LATE)
         value_copy(last_unit)
         value_pool(last_unit)
-        finish_key(0)
         add_rows(last_unit - 1)
         for call in extra[0:2]:
             call()
@@ -536,9 +545,10 @@ def tile_afnb_pa_t_kernel(
         add_third_column(last_unit - 1)
         for call in extra[4:]:
             call()
-        add_rows(last_unit)
-        add_two_columns(last_unit)
-        add_third_column(last_unit)
+        tiles = [slice(m, m + 1) for m in range(K_TILES)]
+        for add in (add_rows, add_two_columns, add_third_column):
+            for m in tiles:
+                add(last_unit, m)
         for call in block_sums(HALVES - 1) + coarse_sums(1):
             call()
         finish_key(1)

@@ -212,22 +212,22 @@ def tile_afnb_pa_t_kernel(
         bv_row = consts.tile([P, CV], BF16)
         ones = consts.tile([P, P], BF16)
         nc.vector.memset(rows_sb[:], 0.0)
+        nc.vector.memset(bv_row[:], 0.0)
         nc.vector.memset(wv_s[:].bitcast(I32), 0)
         nc.vector.memset(wk_s[:].bitcast(I32), 0)
-        nc.vector.memset(bv_row[:], 0.0)
         nc.vector.memset(ones[:], 1.0)
 
         for n, vector in enumerate(vectors):
             nc.scalar.dma_start(
                 out=rows_sb[K_TILES * n : K_TILES * (n + 1), :], in_=vector.rearrange("(m c) -> m c", m=K_TILES)
             )
+        nc.scalar.dma_start(out=bv_row[0:1, :], in_=bv.rearrange("(o c) -> o c", o=1))
         first_raw = [load_group(0, 0)]
         load_weight(nc, wv_words, wv_scales, wv_w, wv_s)
         first_raw.append(load_group(0, 1))
         load_weight(nc, wk_words, wk_scales, wk_w, wk_s)
-        raws = {0: first_raw, 1: load(1)}
-        nc.sync.dma_start(out=bv_row[0:1, :], in_=bv.rearrange("(o c) -> o c", o=1))
-        for u in range(2, LOOKAHEAD):
+        raws = {0: first_raw}
+        for u in range(1, LOOKAHEAD):
             raws[u] = load(u)
         warm = consts.tile([P, 1], F32)
         nc.scalar.sqrt(out=warm[:], in_=ones[:, 0:1])
@@ -366,13 +366,15 @@ def tile_afnb_pa_t_kernel(
             v_cells[u] = work.tile([P, CV], F32, name="v_cells")
             nc.scalar.copy(out=v_cells[u][:], in_=v_accs[u][:])
 
+        def value_bias():
+            for b in range(B):
+                value_acc[b] = value_psum.tile([P, CV], F32, name="value_acc")
+                nc.tensor.matmul(out=value_acc[b][:], lhsT=ones[:], rhs=bv_row[:], start=True, stop=False)
+
         def value_pool(u):
             for b in range(B):
                 n = u - (UNITS_OF_BATCH - 1) * b
                 if 0 <= n < UNITS_OF_BATCH:
-                    if b not in value_acc:
-                        value_acc[b] = value_psum.tile([P, CV], F32, name="value_acc")
-                        nc.tensor.matmul(out=value_acc[b][:], lhsT=ones[:], rhs=bv_row[:], start=True, stop=False)
                     nc.tensor.matmul(
                         out=value_acc[b][:],
                         lhsT=pool_w[:, UNITS_OF_BATCH * b + n, :],
@@ -409,13 +411,14 @@ def tile_afnb_pa_t_kernel(
                         in1=both_rows[u][:, tiles, 2, cells],
                     )
 
-        def block_sums(h):
+        def block_sums(h, tiles=slice(0, K_TILES)):
             b, half = divmod(h, 2)
             pairs, rows8, rows6 = (
-                work.tile([P, K_TILES, n, SIDE], F32, name=name) for name, n in (("pairs", 4), ("rows8", 4), ("rows6", 3))
+                work.tile([P, tiles.stop - tiles.start, n, SIDE], F32, name=name)
+                for name, n in (("pairs", 4), ("rows8", 4), ("rows6", 3))
             )
-            six = k_cells[h][:].rearrange("p m (i x c) -> p (m i) x c", x=6, c=SIDE)
-            twelve = k_cells[h][:].rearrange("p m (y c) -> p m y c", c=SIDE)
+            six = k_cells[h][:, tiles, :].rearrange("p m (i x c) -> p (m i) x c", x=6, c=SIDE)
+            twelve = k_cells[h][:, tiles, :].rearrange("p m (y c) -> p m y c", c=SIDE)
 
             def by_six(tile):
                 return tile[:].rearrange("p m (i e) c -> p (m i) e c", e=2)
@@ -423,7 +426,7 @@ def tile_afnb_pa_t_kernel(
             def strips(s, rows):
                 n_rows = s // 2
                 nc.vector.tensor_reduce(
-                    out=sums[b][s][:, :, n_rows * half : n_rows * (half + 1), :],
+                    out=sums[b][s][:, tiles, n_rows * half : n_rows * (half + 1), :],
                     in_=rows[:].rearrange("p m i (j k) -> p m i j k", k=SIDE // s),
                     axis=AXIS.X,
                     op=ALU.add,
@@ -434,8 +437,8 @@ def tile_afnb_pa_t_kernel(
                 lambda: nc.vector.tensor_add(out=by_six(rows8), in0=by_six(pairs), in1=six[:, :, 2:4, :]),
                 lambda: nc.vector.tensor_add(out=rows6[:, :, 1, :], in0=pairs[:, :, 1, :], in1=pairs[:, :, 2, :]),
                 lambda: nc.vector.tensor_add(out=rows6[:, :, 0:3:2, :], in0=rows8[:, :, 0:4:3, :], in1=twelve[:, :, 3:9:5, :]),
-                lambda: strips(8, rows8),
                 lambda: strips(6, rows6),
+                lambda: strips(8, rows8),
             ]
 
         def coarse_sums(b):
@@ -457,7 +460,7 @@ def tile_afnb_pa_t_kernel(
         def finish_value(b):
             value_sb = work.tile([P, CV], F32, name="value_sb")
             nc.scalar.copy(out=value_sb[:], in_=value_acc[b][:])
-            nc.sync.dma_start(out=out_0[b], in_=value_sb[0:LOCATIONS, :])
+            nc.scalar.dma_start(out=out_0[b], in_=value_sb[0:LOCATIONS, :])
 
         def finish_key(b):
             key_sb = work.tile([P, K_TILES, LOCATIONS], F32, name="key_sb")
@@ -489,6 +492,8 @@ def tile_afnb_pa_t_kernel(
             if n < 2:
                 quantise(n, LOWER, 0)
                 value_matmuls(n, LOWER, 0)
+            if n == 0:
+                value_bias()
             if n == 1:
                 key_relu(n - 1, EARLY)
                 key_relu(n - 1, LATE)
@@ -505,7 +510,8 @@ def tile_afnb_pa_t_kernel(
                 add_two_columns(n - 2)
             quantise(n, UPPER, 1)
             key_matmuls(n, EARLY)
-            value_matmuls(n, UPPER, 1)
+            if not closing:
+                value_matmuls(n, UPPER, 1)
             for call in extra[0:2]:
                 call()
             if before_last:
@@ -523,6 +529,7 @@ def tile_afnb_pa_t_kernel(
             if last and not closing:
                 value_pool(n - 1)
             if closing:
+                value_matmuls(n, UPPER, 1)
                 value_matmuls(n, LOWER, 0)
             value_matmuls(n, LOWER, 1)
             for call in extra[4:]:
@@ -545,11 +552,13 @@ def tile_afnb_pa_t_kernel(
         add_third_column(last_unit - 1)
         for call in extra[4:]:
             call()
-        tiles = [slice(m, m + 1) for m in range(K_TILES)]
-        for add in (add_rows, add_two_columns, add_third_column):
-            for m in tiles:
-                add(last_unit, m)
-        for call in block_sums(HALVES - 1) + coarse_sums(1):
+        chains = [
+            [lambda add=add, m=m: add(last_unit, slice(m, m + 1)) for add in (add_rows, add_two_columns, add_third_column)]
+            + block_sums(HALVES - 1, slice(m, m + 1))
+            for m in range(K_TILES)
+        ]
+        weave(chains[0], [lambda: None] + chains[1])
+        for call in coarse_sums(1):
             call()
         finish_key(1)
         finish_value(1)

@@ -38,6 +38,8 @@ N_CHUNKS = PAIRS // CHUNK_PAIRS
 UNITS_OF_BATCH = 5
 MAX_PAIRS = 6
 
+VECTOR, SCALAR = 0, 1
+LEAD_FROM = 2
 K_TILES = CK // P
 LOOKAHEAD = 3
 UPPER, LOWER = 0, 1
@@ -212,15 +214,17 @@ def tile_afnb_pa_t_kernel(
         bv_row = consts.tile([P, CV], BF16)
         ones = consts.tile([P, P], BF16)
         nc.vector.memset(rows_sb[:], 0.0)
-        nc.vector.memset(bv_row[:], 0.0)
-        nc.vector.memset(wv_s[:].bitcast(I32), 0)
-        nc.vector.memset(wk_s[:].bitcast(I32), 0)
         nc.vector.memset(ones[:], 1.0)
+        nc.vector.memset(wv_s[:].bitcast(I32), 0)
+        nc.vector.memset(bv_row[:], 0.0)
+        nc.vector.memset(wk_s[:].bitcast(I32), 0)
 
         for n, vector in enumerate(vectors):
             nc.scalar.dma_start(
                 out=rows_sb[K_TILES * n : K_TILES * (n + 1), :], in_=vector.rearrange("(m c) -> m c", m=K_TILES)
             )
+        warm = consts.tile([P, 1], F32)
+        nc.scalar.sqrt(out=warm[:], in_=ones[:, 0:1])
         nc.scalar.dma_start(out=bv_row[0:1, :], in_=bv.rearrange("(o c) -> o c", o=1))
         first_raw = [load_group(0, 0)]
         load_weight(nc, wv_words, wv_scales, wv_w, wv_s)
@@ -229,8 +233,6 @@ def tile_afnb_pa_t_kernel(
         raws = {0: first_raw}
         for u in range(1, LOOKAHEAD):
             raws[u] = load(u)
-        warm = consts.tile([P, 1], F32)
-        nc.scalar.sqrt(out=warm[:], in_=ones[:, 0:1])
 
         pool_w = consts.tile([P, B * UNITS_OF_BATCH, P], F32)
         tables = cell_tables(nc, consts)
@@ -281,15 +283,14 @@ def tile_afnb_pa_t_kernel(
             q, j = divmod(u, CHUNK_UNITS)
             return q, slice(UNIT * j, UNIT * (j + 1))
 
-        def regroup(u, g):
+        def regroup(u, g, engine):
             j = u % CHUNK_UNITS
             lo, hi = first_pair(j), first_pair(j + 1)
-            shares = (
-                (nc.vector.tensor_copy, UPPER, 0, SIDE),
-                (nc.scalar.copy, LOWER, 0, S_CELLS),
-                (nc.vector.tensor_copy, LOWER, S_CELLS, SIDE),
-            )
-            for copy, i_r, c0, c1 in shares:
+            shares = {
+                VECTOR: ((nc.vector.tensor_copy, UPPER, 0, SIDE), (nc.vector.tensor_copy, LOWER, S_CELLS, SIDE)),
+                SCALAR: ((nc.scalar.copy, LOWER, 0, S_CELLS),),
+            }
+            for copy, i_r, c0, c1 in shares[engine]:
                 copy(
                     out=grouped[g][:, CELL_W * i_r : CELL_W * (i_r + 1), SIDE * lo : SIDE * hi, :].rearrange(
                         "p k (r c) t -> p r c t k", c=SIDE
@@ -481,7 +482,13 @@ def tile_afnb_pa_t_kernel(
             closing = n == N_UNITS - 1
             if n + LOOKAHEAD < N_UNITS:
                 raws[n + LOOKAHEAD] = load(n + LOOKAHEAD)
-            regroup(n, 0)
+            regroup(n, 0, VECTOR)
+            if n < LEAD_FROM:
+                regroup(n, 0, SCALAR)
+            else:
+                regroup(n, 1, SCALAR)
+                if not closing:
+                    regroup(n + 1, 0, SCALAR)
             if before_last:
                 add_rows(n - 2)
             quantise(n, UPPER, 0)
@@ -498,7 +505,11 @@ def tile_afnb_pa_t_kernel(
                 key_relu(n - 1, EARLY)
                 key_relu(n - 1, LATE)
                 value_copy(n - 1)
-            regroup(n, 1)
+            regroup(n, 1, VECTOR)
+            if n < LEAD_FROM:
+                regroup(n, 1, SCALAR)
+                if n == LEAD_FROM - 1:
+                    regroup(n + 1, 0, SCALAR)
             if closing:
                 finish_value(0)
                 finish_key(0)
@@ -512,10 +523,12 @@ def tile_afnb_pa_t_kernel(
             key_matmuls(n, EARLY)
             if not closing:
                 value_matmuls(n, UPPER, 1)
-            for call in extra[0:2]:
+            for call in extra[0:1]:
                 call()
             if before_last:
                 add_third_column(n - 2)
+            for call in extra[1:2]:
+                call()
             if n > 1:
                 quantise(n, LOWER, 0)
                 if not closing:
@@ -544,20 +557,18 @@ def tile_afnb_pa_t_kernel(
         value_copy(last_unit)
         value_pool(last_unit)
         add_rows(last_unit - 1)
-        for call in extra[0:2]:
-            call()
+        extra[0]()
         add_two_columns(last_unit - 1)
-        for call in extra[2:4]:
-            call()
+        extra[1]()
         add_third_column(last_unit - 1)
-        for call in extra[4:]:
+        for call in (extra[2], extra[5], extra[3]):
             call()
         chains = [
             [lambda add=add, m=m: add(last_unit, slice(m, m + 1)) for add in (add_rows, add_two_columns, add_third_column)]
             + block_sums(HALVES - 1, slice(m, m + 1))
             for m in range(K_TILES)
         ]
-        weave(chains[0], [lambda: None] + chains[1])
+        weave(chains[0], [extra[4]] + chains[1])
         for call in coarse_sums(1):
             call()
         finish_key(1)

from contextlib import ExitStack

import concourse.mybir as mybir
from concourse.masks import make_identity

F32 = mybir.dt.float32
BF16 = mybir.dt.bfloat16
I32 = mybir.dt.int32
U32 = mybir.dt.uint32
U8 = mybir.dt.uint8
FP8X4 = mybir.dt.float8_e4m3fn_x4
FP4X4 = mybir.dt.float4_e2m1fn_x4
ALU = mybir.AluOpType
ACT = mybir.ActivationFunctionType
AXIS = mybir.AxisListType

B, CL, CK, CV, H, W = 2, 1024, 256, 512, 48, 72
GRIDS = (1, 3, 6, 8)
LOCATIONS = 1 + 9 + 36 + 64
EPS = 1e-5

P = 128
PACK = 4
GROUPS = CL // (P * PACK)

CELL_H, CELL_W = 2, 3
PLANES = CELL_H * CELL_W
SIDE = H // CELL_H
PAIR_PX = CELL_H * W
PAIRS = B * SIDE

UNIT = P
N_UNITS = PAIRS * SIDE // UNIT
CHUNK_PAIRS = 16
CHUNK_CELLS = CHUNK_PAIRS * SIDE
CHUNK_UNITS = CHUNK_CELLS // UNIT
N_CHUNKS = PAIRS // CHUNK_PAIRS
UNITS_OF_BATCH = 5
MAX_PAIRS = 6

VECTOR, SCALAR = 0, 1
LEAD_FROM = 2
K_TILES = CK // P
LOOKAHEAD = 3
UPPER, LOWER = 0, 1
EARLY, LATE = 0, 1
EARLY_PLANES = 2
S_CELLS = 20
HALVES = 2 * B
HALF_CELLS = SIDE * SIDE // 2
HALF_AFTER = {2: 0, 4: 1, 6: 2}
PERIOD = 3

FLOPS = 2 * (CK + CV) * CL * B * H * W


def first_pair(j):
    rows = -(-UNIT * j // SIDE)
    return min(rows + rows % 2, CHUNK_PAIRS)


def load_weight(nc, words, scales, words_sb, scales_sb):
    nc.sync.dma_start(out=words_sb[:].bitcast(I32), in_=words.rearrange("g p n -> p g n").bitcast(I32))
    for quad in range(4):
        nc.sync.dma_start(
            out=scales_sb[32 * quad : 32 * quad + 4].bitcast(I32),
            in_=scales[:, 4 * quad : 4 * quad + 4, :].rearrange("g r n -> r g n").bitcast(I32),
        )


def cell_tables(nc, pool):
    edges_r, edges_c = PAIRS + 1, SIDE + 1
    start = UNIT % SIDE
    most_rows = (P - 1 + start * (PERIOD - 1)) // SIDE
    shifted = pool.tile([P, 2, PERIOD], F32)
    nc.gpsimd.iota(
        shifted[:], pattern=[[0, 2], [start, PERIOD]], base=0, channel_multiplier=1,
        allow_small_or_imprecise_dtypes=True,
    )
    passed = pool.tile([P, 2, PERIOD, most_rows], F32)
    nc.gpsimd.memset(passed[:], 1.0)
    nc.gpsimd.affine_select(
        out=passed[:], in_=passed[:], pattern=[[0, 2], [start, PERIOD], [-SIDE, most_rows]],
        compare_op=ALU.is_ge, fill=0.0, base=-SIDE, channel_multiplier=1,
    )
    col_edge = pool.tile([P, edges_c], F32)
    nc.gpsimd.iota(
        col_edge[:], pattern=[[1, edges_c]], base=0, channel_multiplier=0, allow_small_or_imprecise_dtypes=True
    )
    reached_r = pool.tile([P, N_UNITS, edges_r], F32)
    nc.gpsimd.memset(reached_r[:], 1.0)
    nc.gpsimd.affine_select(
        out=reached_r[:], in_=reached_r[:], pattern=[[UNIT, N_UNITS], [-SIDE, edges_r]],
        compare_op=ALU.is_ge, fill=0.0, base=0, channel_multiplier=1,
    )
    return shifted, passed, col_edge, reached_r


def pool_weight_steps(nc, pool, tables, pool_w):
    shifted, passed, col_edge, reached_r = tables
    edges_c = SIDE + 1
    n_cols = 2 * PERIOD
    row_hot, col_hot = {}, {}

    def make_row_hot(s):
        step = SIDE // s
        row_hot[s] = pool.tile([P, N_UNITS, B * s], F32, name="row_hot%d" % s)
        nc.vector.tensor_sub(
            out=row_hot[s][:], in0=reached_r[:, :, 0:PAIRS:step], in1=reached_r[:, :, step : PAIRS + 1 : step]
        )

    rows_on = pool.tile([P, n_cols], F32)
    nc.vector.tensor_reduce(
        out=rows_on[:], in_=passed[:].rearrange("p a n i -> p (a n) i"), axis=AXIS.X, op=ALU.add
    )
    nc.vector.memset(pool_w[:, :, LOCATIONS:P], 0.0)
    col = pool.tile([P, n_cols], F32)
    nc.vector.scalar_tensor_tensor(
        out=col[:], in0=rows_on[:], scalar=-float(SIDE), in1=shifted[:].rearrange("p a n -> p (a n)"),
        op0=ALU.mult, op1=ALU.add,
    )
    reached_c = pool.tile([P, n_cols, edges_c], F32)
    before_c = pool.tile([P, n_cols, edges_c], F32)
    for steps_c, op in ((reached_c, ALU.is_ge), (before_c, ALU.is_lt)):
        nc.vector.tensor_tensor(
            out=steps_c[:],
            in0=col[:].unsqueeze(2).to_broadcast([P, n_cols, edges_c]),
            in1=col_edge[:].unsqueeze(1).to_broadcast([P, n_cols, edges_c]),
            op=op,
        )
    for s in GRIDS:
        step = SIDE // s
        col_hot[s] = pool.tile([P, n_cols, s], F32, name="col_hot%d" % s)
        nc.vector.scalar_tensor_tensor(
            out=col_hot[s][:],
            in0=reached_c[:, :, 0:SIDE:step],
            scalar=1.0 / ((H // s) * (W // s)),
            in1=before_c[:, :, step : SIDE + 1 : step],
            op0=ALU.mult,
            op1=ALU.mult,
        )
    for s in GRIDS:
        make_row_hot(s)

    def product(s, b, offset):
        first = (UNITS_OF_BATCH - 1) * b
        shape = [P, UNITS_OF_BATCH, s, s]
        nc.vector.tensor_tensor(
            out=pool_w[:, UNITS_OF_BATCH * b : UNITS_OF_BATCH * (b + 1), offset : offset + s * s].rearrange(
                "p u (i j) -> p u i j", j=s
            ),
            in0=row_hot[s][:, first : first + UNITS_OF_BATCH, s * b : s * (b + 1)].unsqueeze(3).to_broadcast(shape),
            in1=col_hot[s][:, first % PERIOD : first % PERIOD + UNITS_OF_BATCH, :].unsqueeze(2).to_broadcast(shape),
            op=ALU.mult,
        )

    steps = []
    offset = 0
    for s in GRIDS:
        for b in range(B):
            steps.append(lambda s=s, b=b, offset=offset: product(s, b, offset))
        offset += s * s
    return steps


def weave(first, second):
    for n in range(max(len(first), len(second))):
        for calls in (first, second):
            if n < len(calls):
                calls[n]()


def tile_afnb_pa_t_kernel(
    tc, low_feats, wk_words, wk_scales, bk, gk, bek, mk, vk, wv_words, wv_scales, bv, out_0, out_1
):
    nc = tc.nc
    with ExitStack() as ctx:
        consts = ctx.enter_context(tc.tile_pool(name="consts", bufs=1))
        raw_pool = ctx.enter_context(tc.tile_pool(name="raw", bufs=LOOKAHEAD + 1))
        work = ctx.enter_context(tc.tile_pool(name="work", bufs=2))
        relu_pool = ctx.enter_context(tc.tile_pool(name="relu", bufs=3))
        k_psum = ctx.enter_context(tc.psum_pool(name="k_psum", bufs=4))
        v_psum = ctx.enter_context(tc.psum_pool(name="v_psum", bufs=2))
        value_psum = ctx.enter_context(tc.psum_pool(name="value_psum", bufs=B))
        ctx.enter_context(tc.manual_schedule())

        x_rows = low_feats.rearrange(
            "b (g p t) (r i) w -> b g p t r (i w)", g=GROUPS, p=P, t=PACK, i=CELL_H
        )

        def load_group(u, g):
            q, j = divmod(u, CHUNK_UNITS)
            first = CHUNK_PAIRS * q + first_pair(j)
            last = CHUNK_PAIRS * q + first_pair(j + 1)
            raw = raw_pool.tile([P, PACK, MAX_PAIRS, PAIR_PX], BF16, name="raw%d" % g)
            for b in range(B):
                lo, hi = max(first, SIDE * b), min(last, SIDE * (b + 1))
                if lo < hi:
                    nc.sync.dma_start(
                        out=raw[:, :, lo - first : hi - first, :],
                        in_=x_rows[b, g, :, :, lo - SIDE * b : hi - SIDE * b, :],
                    )
            return raw

        def load(u):
            return [load_group(u, g) for g in range(GROUPS)]

        wk_w = consts.tile([P, GROUPS, 2 * CK], U8, align_bytes=64)
        wv_w = consts.tile([P, GROUPS, 2 * CV], U8, align_bytes=64)
        wk_s = consts.tile([P, GROUPS, CK], U8, align_bytes=64)
        wv_s = consts.tile([P, GROUPS, CV], U8, align_bytes=64)
        vectors = (bk, gk, bek, mk, vk)
        rows_sb = consts.tile([P, P], BF16)
        bv_row = consts.tile([P, CV], BF16)
        ones = consts.tile([P, P], BF16)
        nc.vector.memset(rows_sb[:], 0.0)
        nc.vector.memset(ones[:], 1.0)
        nc.vector.memset(wv_s[:].bitcast(I32), 0)
        nc.vector.memset(bv_row[:], 0.0)
        nc.vector.memset(wk_s[:].bitcast(I32), 0)

        for n, vector in enumerate(vectors):
            nc.scalar.dma_start(
                out=rows_sb[K_TILES * n : K_TILES * (n + 1), :], in_=vector.rearrange("(m c) -> m c", m=K_TILES)
            )
        warm = consts.tile([P, 1], F32)
        nc.scalar.sqrt(out=warm[:], in_=ones[:, 0:1])
        nc.scalar.dma_start(out=bv_row[0:1, :], in_=bv.rearrange("(o c) -> o c", o=1))
        first_raw = [load_group(0, 0)]
        load_weight(nc, wv_words, wv_scales, wv_w, wv_s)
        first_raw.append(load_group(0, 1))
        load_weight(nc, wk_words, wk_scales, wk_w, wk_s)
        raws = {0: first_raw}
        for u in range(1, LOOKAHEAD):
            raws[u] = load(u)

        pool_w = consts.tile([P, B * UNITS_OF_BATCH, P], F32)
        tables = cell_tables(nc, consts)
        identity = consts.tile([P, P], BF16)
        make_identity(nc, identity[:])
        pool_products = pool_weight_steps(nc, consts, tables, pool_w)

        cols_ps = k_psum.tile([P, P], BF16, name="cols_ps", tag="k_acc")
        nc.tensor.transpose(out=cols_ps[:], in_=rows_sb[:], identity=identity[:])

        std = consts.tile([P, K_TILES], F32)
        gain = consts.tile([P, K_TILES], F32)
        shift = consts.tile([P, K_TILES], F32)
        cols = consts.tile([P, len(vectors), K_TILES], F32)
        inv_std = consts.tile([P, K_TILES], F32)
        centred = consts.tile([P, K_TILES], F32)
        scaled = consts.tile([P, K_TILES], F32)
        bk_c, gk_c, bek_c, mk_c = (cols[:, n, :] for n in range(4))

        def standard_deviation():
            vk_at = K_TILES * (len(vectors) - 1)
            nc.scalar.activation(out=std[:], in_=cols_ps[:, vk_at : vk_at + K_TILES], func=ACT.Sqrt, bias=EPS)

        def small_vectors_out():
            nc.scalar.copy(out=cols[:].rearrange("p n m -> p (n m)"), in_=cols_ps[:, 0 : len(vectors) * K_TILES])
            standard_deviation()
            nc.gpsimd.tensor_sub(out=centred[:], in0=bk_c, in1=mk_c)

        def gain_and_shift():
            nc.vector.reciprocal(out=inv_std[:], in_=std[:])
            nc.gpsimd.tensor_mul(out=gain[:], in0=gk_c, in1=inv_std[:])
            nc.gpsimd.tensor_mul(out=scaled[:], in0=centred[:], in1=gain[:])
            nc.gpsimd.tensor_add(out=shift[:], in0=scaled[:], in1=bek_c)

        grouped = [
            consts.tile([P, PLANES, CHUNK_CELLS, PACK], BF16, name="grouped%d" % g, align_bytes=64)
            for g in range(GROUPS)
        ]
        codes = consts.tile([P, GROUPS, N_UNITS, PLANES, UNIT], U32, align_bytes=64)
        x_scales = consts.tile([P, GROUPS, N_UNITS, PLANES, UNIT], U8, align_bytes=64)
        k_cells = [consts.tile([P, K_TILES, HALF_CELLS], F32, name="k_cells%d" % h) for h in range(HALVES)]
        sums = [
            {s: consts.tile([P, K_TILES, s, s], F32, name="sums%d_%d" % (s, b)) for s in GRIDS} for b in range(B)
        ]
        k_accs, relus, both_rows, two_cols, v_accs, v_cells, value_acc = {}, {}, {}, {}, {}, {}, {}

        def where(u):
            q, j = divmod(u, CHUNK_UNITS)
            return q, slice(UNIT * j, UNIT * (j + 1))

        def regroup(u, g, engine):
            j = u % CHUNK_UNITS
            lo, hi = first_pair(j), first_pair(j + 1)
            shares = {
                VECTOR: ((nc.vector.tensor_copy, UPPER, 0, SIDE), (nc.vector.tensor_copy, LOWER, S_CELLS, SIDE)),
                SCALAR: ((nc.scalar.copy, LOWER, 0, S_CELLS),),
            }
            for copy, i_r, c0, c1 in shares[engine]:
                copy(
                    out=grouped[g][:, CELL_W * i_r : CELL_W * (i_r + 1), SIDE * lo : SIDE * hi, :].rearrange(
                        "p k (r c) t -> p r c t k", c=SIDE
                    )[:, :, c0:c1, :, :],
                    in_=raws[u][g][:, :, 0 : hi - lo, W * i_r : W * (i_r + 1)].rearrange(
                        "p t r (c k) -> p r c t k", k=CELL_W
                    )[:, :, c0:c1, :, :],
                )

        def quantise(u, i_r, g):
            q, unit = where(u)
            for i in range(CELL_W * i_r, CELL_W * (i_r + 1)):
                nc.vector.quantize_mx(
                    out=codes[:, g, u, i, :].bitcast(FP8X4),
                    scales=x_scales[:, g, u, i, :],
                    in_=grouped[g][:, i, unit, :].rearrange("p c t -> p (c t)"),
                )

        def key_pass(out, u, m, g, planes):
            nc.tensor.matmul_mx(
                out=out,
                lhsT=wk_w[:, g, 2 * P * m : 2 * P * (m + 1)].bitcast(FP4X4),
                lhsT_scale=wk_s[:, g, P * m : P * (m + 1)],
                rhs=codes[:, g, u, planes, :].rearrange("p k c -> p (k c)").bitcast(FP8X4),
                rhs_scale=x_scales[:, g, u, planes, :].rearrange("p k c -> p (k c)"),
                start=(g == 0),
                stop=(g == GROUPS - 1),
            )

        def key_matmuls(u, step):
            if step == EARLY:
                k_acc = k_psum.tile([P, K_TILES, EARLY_PLANES, UNIT], F32, name="k_acc")
                for m in range(K_TILES):
                    for i in range(EARLY_PLANES):
                        for g in range(GROUPS):
                            key_pass(k_acc[:, m, i, :], u, m, g, slice(i, i + 1))
                    k_accs[u, step, m] = k_acc[:, m, :, :]
            else:
                for m in range(K_TILES):
                    k_acc = k_psum.tile([P, PLANES - EARLY_PLANES, UNIT], F32, name="k_acc")
                    for g in range(GROUPS):
                        key_pass(k_acc[:].rearrange("p k c -> p (k c)"), u, m, g, slice(EARLY_PLANES, PLANES))
                    k_accs[u, step, m] = k_acc[:]

        def key_relu(u, step):
            if step == EARLY:
                relus[u] = relu_pool.tile([P, K_TILES, PLANES, UNIT], F32, name="relu")
            planes = slice(0, EARLY_PLANES) if step == EARLY else slice(EARLY_PLANES, PLANES)
            for m in range(K_TILES):
                nc.scalar.activation(
                    out=relus[u][:, m, planes, :],
                    in_=k_accs[u, step, m],
                    func=ACT.Relu,
                    bias=shift[:, m : m + 1],
                    scale=gain[:, m : m + 1],
                )

        def value_matmuls(u, i_r, g):
            if i_r == UPPER and g == 0:
                v_accs[u] = v_psum.tile([P, CV], F32, name="v_acc")
            for i_c in range(CELL_W):
                i = CELL_W * i_r + i_c
                nc.tensor.matmul_mx(
                    out=v_accs[u][:],
                    lhsT=codes[:, g, u, i, :].bitcast(FP8X4),
                    lhsT_scale=x_scales[:, g, u, i, :],
                    rhs=wv_w[:, g, :].bitcast(FP4X4),
                    rhs_scale=wv_s[:, g, :],
                    start=(i_r == UPPER and g == 0 and i_c == 0),
                    stop=(i_r == LOWER and g == GROUPS - 1 and i_c == CELL_W - 1),
                )

        def value_copy(u):
            v_cells[u] = work.tile([P, CV], F32, name="v_cells")
            nc.scalar.copy(out=v_cells[u][:], in_=v_accs[u][:])

        def value_bias():
            for b in range(B):
                value_acc[b] = value_psum.tile([P, CV], F32, name="value_acc")
                nc.tensor.matmul(out=value_acc[b][:], lhsT=ones[:], rhs=bv_row[:], start=True, stop=False)

        def value_pool(u):
            for b in range(B):
                n = u - (UNITS_OF_BATCH - 1) * b
                if 0 <= n < UNITS_OF_BATCH:
                    nc.tensor.matmul(
                        out=value_acc[b][:],
                        lhsT=pool_w[:, UNITS_OF_BATCH * b + n, :],
                        rhs=v_cells[u][:],
                        start=False,
                        stop=(n == UNITS_OF_BATCH - 1),
                    )

        def add_rows(u, tiles=slice(0, K_TILES)):
            if u not in both_rows:
                both_rows[u] = work.tile([P, K_TILES, CELL_W, UNIT], F32, name="both_rows")
            nc.vector.tensor_add(
                out=both_rows[u][:, tiles, :, :],
                in0=relus[u][:, tiles, 0:CELL_W, :],
                in1=relus[u][:, tiles, CELL_W:PLANES, :],
            )

        def add_two_columns(u, tiles=slice(0, K_TILES)):
            if u not in two_cols:
                two_cols[u] = work.tile([P, K_TILES, UNIT], F32, name="two_cols")
            nc.vector.tensor_add(
                out=two_cols[u][:, tiles, :], in0=both_rows[u][:, tiles, 0, :], in1=both_rows[u][:, tiles, 1, :]
            )

        def add_third_column(u, tiles=slice(0, K_TILES)):
            for h in range(HALVES):
                first = UNIT * u - HALF_CELLS * h
                lo, hi = max(first, 0), min(first + UNIT, HALF_CELLS)
                if lo < hi:
                    cells = slice(lo - first, hi - first)
                    nc.vector.tensor_add(
                        out=k_cells[h][:, tiles, lo:hi],
                        in0=two_cols[u][:, tiles, cells],
                        in1=both_rows[u][:, tiles, 2, cells],
                    )

        def block_sums(h, tiles=slice(0, K_TILES)):
            b, half = divmod(h, 2)
            pairs, rows8, rows6 = (
                work.tile([P, tiles.stop - tiles.start, n, SIDE], F32, name=name)
                for name, n in (("pairs", 4), ("rows8", 4), ("rows6", 3))
            )
            six = k_cells[h][:, tiles, :].rearrange("p m (i x c) -> p (m i) x c", x=6, c=SIDE)
            twelve = k_cells[h][:, tiles, :].rearrange("p m (y c) -> p m y c", c=SIDE)

            def by_six(tile):
                return tile[:].rearrange("p m (i e) c -> p (m i) e c", e=2)

            def strips(s, rows):
                n_rows = s // 2
                nc.vector.tensor_reduce(
                    out=sums[b][s][:, tiles, n_rows * half : n_rows * (half + 1), :],
                    in_=rows[:].rearrange("p m i (j k) -> p m i j k", k=SIDE // s),
                    axis=AXIS.X,
                    op=ALU.add,
                )

            return [
                lambda: nc.vector.tensor_add(out=by_six(pairs), in0=six[:, :, 0:6:4, :], in1=six[:, :, 1:6:4, :]),
                lambda: nc.vector.tensor_add(out=by_six(rows8), in0=by_six(pairs), in1=six[:, :, 2:4, :]),
                lambda: nc.vector.tensor_add(out=rows6[:, :, 1, :], in0=pairs[:, :, 1, :], in1=pairs[:, :, 2, :]),
                lambda: nc.vector.tensor_add(out=rows6[:, :, 0:3:2, :], in0=rows8[:, :, 0:4:3, :], in1=twelve[:, :, 3:9:5, :]),
                lambda: strips(6, rows6),
                lambda: strips(8, rows8),
            ]

        def coarse_sums(b):
            return [
                lambda: nc.vector.tensor_reduce(
                    out=sums[b][3][:].rearrange("p m i j -> p (m i) j"),
                    in_=sums[b][6][:].rearrange("p m (i a) (j c) -> p (m i) j a c", a=2, c=2),
                    axis=AXIS.XY,
                    op=ALU.add,
                ),
                lambda: nc.vector.tensor_reduce(
                    out=sums[b][1][:].rearrange("p m i j -> p (m i j)"),
                    in_=sums[b][6][:].rearrange("p m i j -> p m (i j)"),
                    axis=AXIS.X,
                    op=ALU.add,
                ),
            ]

        def finish_value(b):
            value_sb = work.tile([P, CV], F32, name="value_sb")
            nc.scalar.copy(out=value_sb[:], in_=value_acc[b][:])
            nc.scalar.dma_start(out=out_0[b], in_=value_sb[0:LOCATIONS, :])

        def finish_key(b):
            key_sb = work.tile([P, K_TILES, LOCATIONS], F32, name="key_sb")
            offsets = {s: sum(c * c for c in GRIDS[: GRIDS.index(s)]) for s in GRIDS}
            for s in (6, 8, 3, 1):
                nc.scalar.mul(
                    out=key_sb[:, :, offsets[s] : offsets[s] + s * s],
                    in_=sums[b][s][:].rearrange("p m i j -> p m (i j)"),
                    mul=1.0 / ((H // s) * (W // s)),
                )
            nc.sync.dma_start(out=out_1[b].rearrange("(m c) l -> c m l", m=K_TILES), in_=key_sb[:])

        small_vectors_out()

        extra = []
        for n in range(N_UNITS):
            last, before_last = n >= 1, n >= 2
            closing = n == N_UNITS - 1
            if n + LOOKAHEAD < N_UNITS:
                raws[n + LOOKAHEAD] = load(n + LOOKAHEAD)
            regroup(n, 0, VECTOR)
            if n < LEAD_FROM:
                regroup(n, 0, SCALAR)
            else:
                regroup(n, 1, SCALAR)
                if not closing:
                    regroup(n + 1, 0, SCALAR)
            if before_last:
                add_rows(n - 2)
            quantise(n, UPPER, 0)
            value_matmuls(n, UPPER, 0)
            if n == 0:
                gain_and_shift()
                weave(pool_products[0:4], [])
            if n < 2:
                quantise(n, LOWER, 0)
                value_matmuls(n, LOWER, 0)
            if n == 0:
                value_bias()
            if n == 1:
                key_relu(n - 1, EARLY)
                key_relu(n - 1, LATE)
                value_copy(n - 1)
            regroup(n, 1, VECTOR)
            if n < LEAD_FROM:
                regroup(n, 1, SCALAR)
                if n == LEAD_FROM - 1:
                    regroup(n + 1, 0, SCALAR)
            if closing:
                finish_value(0)
                finish_key(0)
            if n > 1:
                key_relu(n - 1, EARLY)
                key_relu(n - 1, LATE)
                value_copy(n - 1)
            if before_last:
                add_two_columns(n - 2)
            quantise(n, UPPER, 1)
            key_matmuls(n, EARLY)
            if not closing:
                value_matmuls(n, UPPER, 1)
            for call in extra[0:1]:
                call()
            if before_last:
                add_third_column(n - 2)
            for call in extra[1:2]:
                call()
            if n > 1:
                quantise(n, LOWER, 0)
                if not closing:
                    value_matmuls(n, LOWER, 0)
            for call in extra[2:4]:
                call()
            quantise(n, LOWER, 1)
            key_matmuls(n, LATE)
            if n == 0:
                weave(pool_products[4:], [])
            if last and not closing:
                value_pool(n - 1)
            if closing:
                value_matmuls(n, UPPER, 1)
                value_matmuls(n, LOWER, 0)
            value_matmuls(n, LOWER, 1)
            for call in extra[4:]:
                call()
            extra = block_sums(HALF_AFTER[n - 2]) if n - 2 in HALF_AFTER else []
            if n - 2 == 4:
                extra += coarse_sums(0)
        last_unit = N_UNITS - 1
        value_pool(last_unit - 1)
        key_relu(last_unit, EARLY)
        key_relu(last_unit, LATE)
        value_copy(last_unit)
        value_pool(last_unit)
        add_rows(last_unit - 1)
        extra[0]()
        add_two_columns(last_unit - 1)
        extra[1]()
        add_third_column(last_unit - 1)
        for call in (extra[2], extra[5], extra[3]):
            call()
        chains = [
            [lambda add=add, m=m: add(last_unit, slice(m, m + 1)) for add in (add_rows, add_two_columns, add_third_column)]
            + block_sums(HALVES - 1, slice(m, m + 1))
            for m in range(K_TILES)
        ]
        weave(chains[0], [extra[4]] + chains[1])
        for call in coarse_sums(1):
            call()
        finish_key(1)
        finish_value(1)
